import numpy as np
import ml_dtypes


def mxq(x, axis, fmt="e4m3"):
    dtype, down = {"e4m3": (ml_dtypes.float8_e4m3fn, 7), "e5m2": (ml_dtypes.float8_e5m2, 14)}[fmt]
    v = np.moveaxis(np.asarray(x, np.float32).astype(ml_dtypes.bfloat16).astype(np.float64), axis, -1)
    blocks = v.reshape(v.shape[:-1] + (-1, 32))
    amax = np.abs(blocks).max(-1, keepdims=True)
    byte = np.maximum(np.where(amax > 0, np.frexp(amax)[1] - 1 + 127, 0) - down, 1)
    scale = np.exp2(byte - 127.0)
    codes = (blocks / scale).astype(np.float32).astype(dtype).astype(np.float64)
    return np.moveaxis((codes * scale).reshape(v.shape), -1, axis)


WIDE = False


def mx_kscale(k):
    if not WIDE:
        return np.ones(k)
    levels = np.array([10, -10, 5, -5, 0])
    a = np.random.permutation(np.resize(levels, k // 512 * 4)).reshape(k // 512, 4)
    idx = np.arange(k)
    return np.exp2(a[idx // 512, idx % 128 // 32])


BF16 = ml_dtypes.bfloat16


def bf(x):
    return np.asarray(x, np.float32).astype(BF16)


def f64(x):
    return np.asarray(x).astype(np.float64)


E2M1 = np.array([0.0, 0.5, 1.0, 1.5, 2.0, 3.0, 4.0, 6.0, -0.0, -0.5, -1.0, -1.5, -2.0, -3.0, -4.0, -6.0])


def pack_weight(w, fmt):
    k, n = w.shape
    w = f64(bf(w)).reshape(k // 32, 32, n)
    amax = np.abs(w).max(1)
    if fmt == "e4m3":
        byte = np.frexp(amax)[1] - 1 + 127 - 7
    else:
        mant, ex = np.frexp(amax / 6.0)
        byte = np.where(mant > 0.5, ex, ex - 1) + 127
    byte = np.clip(np.where(amax > 0, byte, 1), 1, 254)
    scaled = (w * np.exp2(127.0 - byte)[:, None, :]).reshape(k, n).astype(np.float32)
    by_word = np.ascontiguousarray(scaled.reshape(k // 512, 128, 4, n).transpose(0, 1, 3, 2))
    if fmt == "e4m3":
        words = by_word.astype(ml_dtypes.float8_e4m3fn).view(np.uint8)
    else:
        c = by_word.astype(ml_dtypes.float4_e2m1fn).view(np.uint8) & 0xF
        words = c[..., 0::2] | (c[..., 1::2] << 4)
    return np.ascontiguousarray(words), np.ascontiguousarray(byte.astype(np.uint8).reshape(k // 512, 16, n))


def unpack_weight(words, scales, fmt):
    g, p, n, _ = words.shape
    if fmt == "e4m3":
        vals = np.ascontiguousarray(words).view(ml_dtypes.float8_e4m3fn).astype(np.float64)
    else:
        nib = np.empty((g, p, n, 4), np.uint8)
        nib[..., 0::2] = words & 0xF
        nib[..., 1::2] = words >> 4
        vals = E2M1[nib]
    vals = vals * np.repeat(np.exp2(scales.astype(np.float64) - 127.0), 8, axis=1)[..., None]
    return vals.transpose(0, 1, 3, 2).reshape(g * 512, n)


T, B, D, U, V, E = 4, 8192, 1024, 16, 512, 8
G = 2 * E
GS = (T + 1) * E
N = U * E


def softmax(v):
    e = np.exp(v - v.max(-1, keepdims=True))
    return e / e.sum(-1, keepdims=True)


def setup_inputs():
    rn = np.random.standard_normal
    s = mx_kscale(D)
    x = bf(rn((B, D)) * s)
    ews0_words, ews0_scales = pack_weight((rn((D, U, E)) / np.sqrt(D) / s[:, None, None]).reshape(D, N), "e4m3")
    ebs0 = bf(rn((U, E)) * 0.5)
    stack = (rn((T, D, U, E)) / np.sqrt(D) / s[None, :, None, None]).reshape(T, D, N)
    ew0_words, ew0_scales = pack_weight(stack.reshape(-1, N), "e4m3")
    return {
        "x": x,
        "ews0_words": ews0_words,
        "ews0_scales": ews0_scales,
        "ebs0": ebs0,
        "ew0_words": ew0_words,
        "ew0_scales": ew0_scales,
        "eb0": bf(rn((T, U, E)) * 0.5),
        "gate_pre0": bf(rn((T, B, G))),
        "gb0": bf(rn((T, G)) * 0.5),
        "sgate_pre": bf(rn((B, GS))),
        "gbs": bf(rn((GS,)) * 0.5),
    }


def reference(x, ews0_words, ews0_scales, ebs0, ew0_words, ew0_scales, eb0, gate_pre0, gb0, sgate_pre, gbs):
    xq = mxq(f64(x), 1, "e4m3")
    es = np.maximum((xq @ unpack_weight(ews0_words, ews0_scales, "e4m3")).reshape(B, U, E) + f64(ebs0), 0.0)
    et = np.maximum((xq @ unpack_weight(ew0_words, ew0_scales, "e4m3").reshape(T, D, N)).reshape(T, B, U, E) + f64(eb0)[:, None], 0.0)
    g = softmax(f64(gate_pre0) + f64(gb0)[:, None])
    comb = np.concatenate([et, np.broadcast_to(es, et.shape)], axis=-1)
    task_out = (comb * g[:, :, None, :]).sum(-1)
    gs = softmax(f64(sgate_pre) + f64(gbs))
    all_exp = np.concatenate([np.moveaxis(et, 0, 2).reshape(B, U, T * E), es], axis=-1)
    share_out = (all_exp * gs[:, None, :]).sum(-1)
    return task_out, share_out

@@ -1,0 +1,333 @@
+from contextlib import ExitStack
+
+import concourse.mybir as mybir
+from concourse.masks import make_identity
+
+F32 = mybir.dt.float32
+BF16 = mybir.dt.bfloat16
+I32 = mybir.dt.int32
+U32 = mybir.dt.uint32
+U8 = mybir.dt.uint8
+FP8X4 = mybir.dt.float8_e4m3fn_x4
+ADD = mybir.AluOpType.add
+MULT = mybir.AluOpType.mult
+MAX = mybir.AluOpType.max
+LAST_AXIS = mybir.AxisListType.X
+EXP = mybir.ActivationFunctionType.Exp
+RELU = mybir.ActivationFunctionType.Relu
+
+P = 128
+TASKS, ROWS, D, UNITS, EXPERTS = 4, 8192, 1024, 16, 8
+GROUPS = TASKS + 1
+SHARED = TASKS
+N = UNITS * EXPERTS
+K_PASS = 4 * P
+PASSES = D // K_PASS
+WORD_PLANES = 2
+TILES = 4
+CHUNK = TILES * P
+CHUNKS = ROWS // CHUNK
+ROWS_PER_PARTITION = ROWS // P
+TASK_GATE = 2 * EXPERTS
+SHARE_GATE = GROUPS * EXPERTS
+TASK_COLS = TASKS * TILES * TASK_GATE
+GATE_COLS = TASK_COLS + TILES * SHARE_GATE
+SOFTMAXES = TASKS * TILES + TILES
+OUT_COLS = TILES * UNITS
+
+FLOPS = 2 * ROWS * D * GROUPS * N
+
+
+def tile_plelayer_pa_t_e_kernel(
+    tc, x, ews0_words, ews0_scales, ebs0, ew0_words, ew0_scales, eb0, gate_pre0, gb0, sgate_pre, gbs, out_0, out_1
+):
+    nc = tc.nc
+    with ExitStack() as ctx:
+        const = ctx.enter_context(tc.tile_pool(name="const", bufs=1))
+        x_pool = ctx.enter_context(tc.tile_pool(name="x_pool", bufs=3))
+        mx_pool = ctx.enter_context(tc.tile_pool(name="mx_pool", bufs=2))
+        hidden_pool = ctx.enter_context(tc.tile_pool(name="hidden_pool", bufs=3))
+        gate_pool = ctx.enter_context(tc.tile_pool(name="gate_pool", bufs=3))
+        sum_pool = ctx.enter_context(tc.tile_pool(name="sum_pool", bufs=2))
+        psum = ctx.enter_context(tc.psum_pool(name="psum", bufs=1))
+
+        ident_f32 = const.tile([P, P], F32)
+        make_identity(nc, ident_f32[:])
+        ident_bf16 = const.tile([P, P], BF16)
+        make_identity(nc, ident_bf16[:])
+        ones_bf16 = const.tile([P, P], BF16)
+        nc.vector.memset(ones_bf16[:], 1.0)
+        expert_major = const.tile([P, P], F32)
+        nc.vector.tensor_copy(
+            out=expert_major[:].rearrange("p (e u) -> p e u", e=EXPERTS),
+            in_=ident_f32[:].rearrange("p (u e) -> p e u", e=EXPERTS),
+        )
+
+        w_codes = const.tile([P, PASSES, GROUPS, N], U32, align_bytes=64)
+        task_words = ew0_words.rearrange("(t g) p n b -> g p t (n b)", g=PASSES).bitcast(I32)
+        for g in range(PASSES):
+            nc.sync.dma_start(out=w_codes[:, g, 0:TASKS, :].bitcast(I32), in_=task_words[g])
+        nc.sync.dma_start(
+            out=w_codes[:, :, SHARED, :].bitcast(I32), in_=ews0_words.rearrange("g p n b -> p g (n b)").bitcast(I32)
+        )
+        w_scales = const.tile([P, PASSES, GROUPS, N], U8, align_bytes=64)
+        w_scales_i32 = w_scales[:].bitcast(I32)
+        nc.vector.memset(w_scales_i32, 0)
+        task_scales = ew0_scales.rearrange("(t g) q n -> g q t n", g=PASSES).bitcast(I32)
+        shared_scales = ews0_scales.rearrange("g q n -> q g n").bitcast(I32)
+        for quadrant in range(4):
+            live = slice(32 * quadrant, 32 * quadrant + 4)
+            rows = slice(4 * quadrant, 4 * quadrant + 4)
+            for g in range(PASSES):
+                nc.sync.dma_start(out=w_scales_i32[live, g, 0:TASKS, :], in_=task_scales[g, rows])
+            nc.sync.dma_start(out=w_scales_i32[live, :, SHARED, :], in_=shared_scales[rows])
+
+        bias_rows = const.tile([P, P], BF16)
+        nc.vector.memset(bias_rows[:], 0.0)
+        nc.sync.dma_start(out=bias_rows[0:TASKS, :], in_=eb0.rearrange("t u e -> t (u e)"))
+        nc.sync.dma_start(out=bias_rows[SHARED : SHARED + 1, :], in_=ebs0.rearrange("u e -> (u e)").unsqueeze(0))
+        bias_columns = psum.tile([P, P], BF16, tag="logits")
+        nc.tensor.transpose(out=bias_columns[:], in_=bias_rows[:], identity=ident_bf16[:])
+        expert_bias = const.tile([P, GROUPS], F32)
+        nc.vector.tensor_copy(out=expert_bias[:], in_=bias_columns[:, 0:GROUPS])
+
+        bias_once = const.tile([1, TASKS * TASK_GATE + SHARE_GATE], BF16)
+        nc.sync.dma_start(out=bias_once[:, 0 : TASKS * TASK_GATE], in_=gb0.rearrange("t s -> (t s)").unsqueeze(0))
+        nc.sync.dma_start(out=bias_once[:, TASKS * TASK_GATE :], in_=gbs.unsqueeze(0))
+        gate_bias = const.tile([P, GATE_COLS], BF16)
+        nc.vector.memset(gate_bias[:], 0.0)
+        nc.vector.tensor_copy(
+            out=gate_bias[0:1, 0:TASK_COLS].rearrange("o (t i s) -> o t i s", t=TASKS, i=TILES),
+            in_=bias_once[:, 0 : TASKS * TASK_GATE]
+            .rearrange("o (t s) -> o t s", t=TASKS)
+            .unsqueeze(2)
+            .to_broadcast([1, TASKS, TILES, TASK_GATE]),
+        )
+        nc.vector.tensor_copy(
+            out=gate_bias[0:1, TASK_COLS:GATE_COLS].rearrange("o (i s) -> o i s", i=TILES),
+            in_=bias_once[:, TASKS * TASK_GATE :].unsqueeze(1).to_broadcast([1, TILES, SHARE_GATE]),
+        )
+
+        gate_pre = const.tile([P, CHUNKS, GATE_COLS], BF16)
+        for t in range(TASKS):
+            nc.sync.dma_start(
+                out=gate_pre[:, :, TILES * TASK_GATE * t : TILES * TASK_GATE * (t + 1)],
+                in_=gate_pre0[t].rearrange("(p c i) s -> p c (i s)", c=CHUNKS, i=TILES),
+            )
+        nc.sync.dma_start(
+            out=gate_pre[:, :, TASK_COLS:GATE_COLS],
+            in_=sgate_pre.rearrange("(p c i) s -> p c (i s)", c=CHUNKS, i=TILES),
+        )
+
+        x_by_partition = x.rearrange("(p a) k -> p a k", a=ROWS_PER_PARTITION)
+        task_out_by_partition = out_0.rearrange("t (p a) u -> p t a u", a=ROWS_PER_PARTITION)
+        share_out_by_partition = out_1.rearrange("(p a) u -> p a u", a=ROWS_PER_PARTITION)
+
+        x_rows, grouped, x_codes, x_scales, hidden = {}, {}, {}, {}, {}
+        gates, inverse_sums, task_products, share_products, task_quarters, share_quarters = {}, {}, {}, {}, {}, {}
+
+        def load_x(c):
+            rows = x_pool.tile([P, TILES, D], BF16)
+            nc.sync.dma_start(out=rows[:], in_=x_by_partition[:, TILES * c : TILES * (c + 1), :])
+            x_rows[c] = rows
+
+        def transpose_x(c, i):
+            if i == 0:
+                side_by_side = mx_pool.tile([P, PASSES * CHUNK * 4], BF16, align_bytes=64)
+                grouped[c] = side_by_side
+            words = x_rows[c][:, i, :].bitcast(F32)
+            flipped = psum.tile([P, PASSES * WORD_PLANES, P], F32, tag="flipped", bufs=2)
+            for g in range(PASSES):
+                for h in range(WORD_PLANES):
+                    first = (K_PASS // 2) * g + h
+                    nc.tensor.transpose(
+                        out=flipped[:, WORD_PLANES * g + h, :],
+                        in_=words[:, first : (K_PASS // 2) * (g + 1) : WORD_PLANES],
+                        identity=ident_f32[:],
+                    )
+            nc.scalar.copy(
+                out=grouped[c][:]
+                .bitcast(F32)
+                .rearrange("p (g n h) -> p g n h", g=PASSES, h=WORD_PLANES)[:, :, P * i : P * (i + 1), :],
+                in_=flipped[:].rearrange("p (g h) n -> p g n h", h=WORD_PLANES),
+            )
+
+        def quantise_x(c):
+            codes = mx_pool.tile([P, PASSES * CHUNK], U32, align_bytes=64)
+            scales = mx_pool.tile([P, PASSES * CHUNK], U8, align_bytes=64)
+            nc.vector.quantize_mx(out=codes[:].bitcast(FP8X4), scales=scales[:], in_=grouped[c][:])
+            x_codes[c] = codes
+            x_scales[c] = scales
+
+        def run_experts(c, w):
+            z = psum.tile([P, CHUNK], F32, tag="z", bufs=2)
+            for g in range(PASSES):
+                columns = slice(CHUNK * g, CHUNK * (g + 1))
+                nc.tensor.matmul_mx(
+                    out=z[:],
+                    lhsT=w_codes[:, g, w, :].bitcast(FP8X4),
+                    lhsT_scale=w_scales[:, g, w, :],
+                    rhs=x_codes[c][:, columns].bitcast(FP8X4),
+                    rhs_scale=x_scales[c][:, columns],
+                    start=(g == 0),
+                    stop=(g == PASSES - 1),
+                )
+            active = hidden_pool.tile([P, CHUNK], F32)
+            nc.scalar.activation(out=active[:], in_=z[:], func=RELU, bias=expert_bias[:, w : w + 1], scale=1.0)
+            hidden[c, w] = active
+
+        def softmax_gates(c):
+            logits = psum.tile([P, GATE_COLS], F32, tag="logits")
+            nc.tensor.matmul(out=logits[:], lhsT=ones_bf16[:], rhs=gate_bias[:], start=True, stop=False)
+            nc.tensor.matmul(out=logits[:], lhsT=ident_bf16[:], rhs=gate_pre[:, c, :], start=False, stop=True)
+            max_of_8 = gate_pool.tile([P, GATE_COLS // EXPERTS], F32)
+            nc.vector.tensor_reduce(
+                out=max_of_8[:], in_=logits[:].rearrange("p (a e) -> p a e", e=EXPERTS), axis=LAST_AXIS, op=MAX
+            )
+            minus_max = gate_pool.tile([P, SOFTMAXES], F32)
+            split = TASK_COLS // EXPERTS
+            nc.vector.tensor_reduce(
+                out=minus_max[:, 0 : TASKS * TILES],
+                in_=max_of_8[:, 0:split].rearrange("p (a h) -> p a h", h=TASK_GATE // EXPERTS),
+                axis=LAST_AXIS,
+                op=MAX,
+                negate=True,
+            )
+            nc.vector.tensor_reduce(
+                out=minus_max[:, TASKS * TILES : SOFTMAXES],
+                in_=max_of_8[:, split:].rearrange("p (a h) -> p a h", h=SHARE_GATE // EXPERTS),
+                axis=LAST_AXIS,
+                op=MAX,
+                negate=True,
+            )
+            weights = gate_pool.tile([P, GATE_COLS], F32)
+            sums = gate_pool.tile([P, SOFTMAXES], F32)
+            for a in range(SOFTMAXES):
+                if a < TASKS * TILES:
+                    columns = slice(TASK_GATE * a, TASK_GATE * (a + 1))
+                else:
+                    first = TASK_COLS + SHARE_GATE * (a - TASKS * TILES)
+                    columns = slice(first, first + SHARE_GATE)
+                nc.scalar.activation(
+                    out=weights[:, columns],
+                    in_=logits[:, columns],
+                    func=EXP,
+                    bias=minus_max[:, a : a + 1],
+                    scale=1.0,
+                    accum_out=sums[:, a : a + 1],
+                )
+            one_over = gate_pool.tile([P, SOFTMAXES], F32)
+            nc.vector.reciprocal(out=one_over[:], in_=sums[:])
+            gates[c] = weights
+            inverse_sums[c] = one_over
+
+        def gate_entries(c, first_col, width, first_entry):
+            by_tile = gates[c][:, first_col : first_col + TILES * width].rearrange("p (i s) -> p i s", s=width)
+            eight = by_tile[:, :, first_entry : first_entry + EXPERTS].rearrange("p i e -> p e i")
+            return eight.unsqueeze(3).to_broadcast([P, EXPERTS, TILES, UNITS])
+
+        def weigh_experts(c, w):
+            if w == 0:
+                for_tasks = sum_pool.tile([P, EXPERTS, 2, TASKS, OUT_COLS], F32)
+                for_share = sum_pool.tile([P, EXPERTS, GROUPS, OUT_COLS], F32)
+                task_products[c] = for_tasks
+                share_products[c] = for_share
+            by_row = psum.tile([P, TILES, N], F32, tag="by_row", bufs=3)
+            for i in range(TILES):
+                nc.tensor.transpose(
+                    out=by_row[:, i, :], in_=hidden[c, w][:, P * i : P * (i + 1)], identity=expert_major[:]
+                )
+            units = by_row[:].rearrange("p i (e u) -> p e i u", e=EXPERTS)
+
+            def product(out, gate):
+                nc.vector.tensor_tensor(
+                    out=out.rearrange("p e (i u) -> p e i u", u=UNITS), in0=units, in1=gate, op=MULT
+                )
+
+            task_width = TILES * TASK_GATE
+            if w == SHARED:
+                for t in range(TASKS):
+                    product(task_products[c][:, :, 1, t, :], gate_entries(c, task_width * t, TASK_GATE, EXPERTS))
+            else:
+                product(task_products[c][:, :, 0, w, :], gate_entries(c, task_width * w, TASK_GATE, 0))
+            product(share_products[c][:, :, w, :], gate_entries(c, TASK_COLS, SHARE_GATE, EXPERTS * w))
+
+        def halve_twice(c):
+            for products, quarters, name in (
+                (task_products[c][:].rearrange("p e k t n -> p e (k t n)"), task_quarters, "task"),
+                (share_products[c][:].rearrange("p e w n -> p e (w n)"), share_quarters, "share"),
+            ):
+                width = products.shape[2]
+                half = sum_pool.tile([P, EXPERTS // 2, width], F32, name=name + "_half")
+                nc.gpsimd.tensor_tensor(
+                    out=half[:], in0=products[:, 0 : EXPERTS // 2, :], in1=products[:, EXPERTS // 2 :, :], op=ADD
+                )
+                quarter = sum_pool.tile([P, EXPERTS // 4, width], F32, name=name + "_quarter")
+                nc.gpsimd.tensor_tensor(
+                    out=quarter[:], in0=half[:, 0 : EXPERTS // 4, :], in1=half[:, EXPERTS // 4 :, :], op=ADD
+                )
+                quarters[c] = quarter
+
+        def finish(c):
+            task_out = sum_pool.tile([P, TASKS, OUT_COLS], F32)
+            nc.vector.tensor_reduce(
+                out=task_out[:],
+                in_=task_quarters[c][:].rearrange("p e (k t n) -> p t n (e k)", k=2, t=TASKS),
+                axis=LAST_AXIS,
+                op=ADD,
+            )
+            share_out = sum_pool.tile([P, OUT_COLS], F32)
+            nc.vector.tensor_reduce(
+                out=share_out[:],
+                in_=share_quarters[c][:].rearrange("p e (w n) -> p n (e w)", w=GROUPS),
+                axis=LAST_AXIS,
+                op=ADD,
+            )
+            one_over = inverse_sums[c]
+            task_view = task_out[:].rearrange("p t (i u) -> p t i u", u=UNITS)
+            nc.vector.tensor_tensor(
+                out=task_view,
+                in0=task_view,
+                in1=one_over[:, 0 : TASKS * TILES]
+                .rearrange("p (t i) -> p t i", t=TASKS)
+                .unsqueeze(3)
+                .to_broadcast([P, TASKS, TILES, UNITS]),
+                op=MULT,
+            )
+            share_view = share_out[:].rearrange("p (i u) -> p i u", u=UNITS)
+            nc.vector.tensor_tensor(
+                out=share_view,
+                in0=share_view,
+                in1=one_over[:, TASKS * TILES : SOFTMAXES].unsqueeze(2).to_broadcast([P, TILES, UNITS]),
+                op=MULT,
+            )
+            own_rows = slice(TILES * c, TILES * (c + 1))
+            nc.sync.dma_start(out=task_out_by_partition[:, :, own_rows, :], in_=task_view)
+            nc.sync.dma_start(out=share_out_by_partition[:, own_rows, :], in_=share_view)
+
+        load_x(0)
+        load_x(1)
+        for i in range(TILES):
+            transpose_x(0, i)
+        softmax_gates(0)
+        quantise_x(0)
+        run_experts(0, 0)
+        for c in range(CHUNKS):
+            more = c + 1 < CHUNKS
+            if c + 2 < CHUNKS:
+                load_x(c + 2)
+            if more:
+                softmax_gates(c + 1)
+            for w in range(GROUPS):
+                if w + 1 < GROUPS:
+                    run_experts(c, w + 1)
+                elif more:
+                    quantise_x(c + 1)
+                    run_experts(c + 1, 0)
+                if more and w < TILES:
+                    transpose_x(c + 1, w)
+                weigh_experts(c, w)
+            halve_twice(c)
+            if c > 0:
+                finish(c - 1)
+        finish(CHUNKS - 1)

@@ -34,6 +34,8 @@ TASK_COLS = TASKS * TILES * TASK_GATE
 GATE_COLS = TASK_COLS + TILES * SHARE_GATE
 SOFTMAXES = TASKS * TILES + TILES
 OUT_COLS = TILES * UNITS
+LEFT = 4
+LAG = 2
 
 FLOPS = 2 * ROWS * D * GROUPS * N
 
@@ -47,7 +49,7 @@ def tile_plelayer_pa_t_e_kernel(
         x_pool = ctx.enter_context(tc.tile_pool(name="x_pool", bufs=3))
         mx_pool = ctx.enter_context(tc.tile_pool(name="mx_pool", bufs=2))
         hidden_pool = ctx.enter_context(tc.tile_pool(name="hidden_pool", bufs=3))
-        gate_pool = ctx.enter_context(tc.tile_pool(name="gate_pool", bufs=3))
+        gate_pool = ctx.enter_context(tc.tile_pool(name="gate_pool", bufs=4))
         sum_pool = ctx.enter_context(tc.tile_pool(name="sum_pool", bufs=2))
         psum = ctx.enter_context(tc.psum_pool(name="psum", bufs=1))
 
@@ -124,7 +126,8 @@ def tile_plelayer_pa_t_e_kernel(
         share_out_by_partition = out_1.rearrange("(p a) u -> p a u", a=ROWS_PER_PARTITION)
 
         x_rows, grouped, x_codes, x_scales, hidden = {}, {}, {}, {}, {}
-        gates, inverse_sums, task_products, share_products, task_quarters, share_quarters = {}, {}, {}, {}, {}, {}
+        logits, minus_max, gates, gate_sums = {}, {}, {}, {}
+        task_products, share_products, task_quarters, share_quarters, task_sums = {}, {}, {}, {}, {}
 
         def load_x(c):
             rows = x_pool.tile([P, TILES, D], BF16)
@@ -176,25 +179,25 @@ def tile_plelayer_pa_t_e_kernel(
             nc.scalar.activation(out=active[:], in_=z[:], func=RELU, bias=expert_bias[:, w : w + 1], scale=1.0)
             hidden[c, w] = active
 
-        def softmax_gates(c):
-            logits = psum.tile([P, GATE_COLS], F32, tag="logits")
-            nc.tensor.matmul(out=logits[:], lhsT=ones_bf16[:], rhs=gate_bias[:], start=True, stop=False)
-            nc.tensor.matmul(out=logits[:], lhsT=ident_bf16[:], rhs=gate_pre[:, c, :], start=False, stop=True)
+        def gate_logits(c):
+            with_bias = psum.tile([P, GATE_COLS], F32, tag="logits")
+            nc.tensor.matmul(out=with_bias[:], lhsT=ones_bf16[:], rhs=gate_bias[:], start=True, stop=False)
+            nc.tensor.matmul(out=with_bias[:], lhsT=ident_bf16[:], rhs=gate_pre[:, c, :], start=False, stop=True)
             max_of_8 = gate_pool.tile([P, GATE_COLS // EXPERTS], F32)
             nc.vector.tensor_reduce(
-                out=max_of_8[:], in_=logits[:].rearrange("p (a e) -> p a e", e=EXPERTS), axis=LAST_AXIS, op=MAX
+                out=max_of_8[:], in_=with_bias[:].rearrange("p (a e) -> p a e", e=EXPERTS), axis=LAST_AXIS, op=MAX
             )
-            minus_max = gate_pool.tile([P, SOFTMAXES], F32)
+            negated = gate_pool.tile([P, SOFTMAXES], F32)
             split = TASK_COLS // EXPERTS
             nc.vector.tensor_reduce(
-                out=minus_max[:, 0 : TASKS * TILES],
+                out=negated[:, 0 : TASKS * TILES],
                 in_=max_of_8[:, 0:split].rearrange("p (a h) -> p a h", h=TASK_GATE // EXPERTS),
                 axis=LAST_AXIS,
                 op=MAX,
                 negate=True,
             )
             nc.vector.tensor_reduce(
-                out=minus_max[:, TASKS * TILES : SOFTMAXES],
+                out=negated[:, TASKS * TILES : SOFTMAXES],
                 in_=max_of_8[:, split:].rearrange("p (a h) -> p a h", h=SHARE_GATE // EXPERTS),
                 axis=LAST_AXIS,
                 op=MAX,
@@ -202,24 +205,21 @@ def tile_plelayer_pa_t_e_kernel(
             )
             weights = gate_pool.tile([P, GATE_COLS], F32)
             sums = gate_pool.tile([P, SOFTMAXES], F32)
-            for a in range(SOFTMAXES):
-                if a < TASKS * TILES:
-                    columns = slice(TASK_GATE * a, TASK_GATE * (a + 1))
-                else:
-                    first = TASK_COLS + SHARE_GATE * (a - TASKS * TILES)
-                    columns = slice(first, first + SHARE_GATE)
+            logits[c], minus_max[c], gates[c], gate_sums[c] = with_bias, negated, weights, sums
+
+        def exponentiate(c, w):
+            width = SHARE_GATE if w == SHARED else TASK_GATE
+            for i in range(TILES):
+                a = TILES * w + i
+                first = TILES * TASK_GATE * w + width * i
                 nc.scalar.activation(
-                    out=weights[:, columns],
-                    in_=logits[:, columns],
+                    out=gates[c][:, first : first + width],
+                    in_=logits[c][:, first : first + width],
                     func=EXP,
-                    bias=minus_max[:, a : a + 1],
+                    bias=minus_max[c][:, a : a + 1],
                     scale=1.0,
-                    accum_out=sums[:, a : a + 1],
+                    accum_out=gate_sums[c][:, a : a + 1],
                 )
-            one_over = gate_pool.tile([P, SOFTMAXES], F32)
-            nc.vector.reciprocal(out=one_over[:], in_=sums[:])
-            gates[c] = weights
-            inverse_sums[c] = one_over
 
         def gate_entries(c, first_col, width, first_entry):
             by_tile = gates[c][:, first_col : first_col + TILES * width].rearrange("p (i s) -> p i s", s=width)
@@ -232,7 +232,7 @@ def tile_plelayer_pa_t_e_kernel(
                 for_share = sum_pool.tile([P, EXPERTS, GROUPS, OUT_COLS], F32)
                 task_products[c] = for_tasks
                 share_products[c] = for_share
-            by_row = psum.tile([P, TILES, N], F32, tag="by_row", bufs=3)
+            by_row = psum.tile([P, TILES, N], F32, tag="by_row", bufs=2)
             for i in range(TILES):
                 nc.tensor.transpose(
                     out=by_row[:, i, :], in_=hidden[c, w][:, P * i : P * (i + 1)], identity=expert_major[:]
@@ -268,66 +268,75 @@ def tile_plelayer_pa_t_e_kernel(
                 )
                 quarters[c] = quarter
 
-        def finish(c):
-            task_out = sum_pool.tile([P, TASKS, OUT_COLS], F32)
-            nc.vector.tensor_reduce(
-                out=task_out[:],
-                in_=task_quarters[c][:].rearrange("p e (k t n) -> p t n (e k)", k=2, t=TASKS),
-                axis=LAST_AXIS,
-                op=ADD,
+        def add_quarter(c, r):
+            if r == 0:
+                totals = psum.tile([P, TASKS * OUT_COLS], F32, tag="task_sums")
+                task_sums[c] = totals
+            slices = task_quarters[c][:].rearrange("p e (k n) -> p (e k) n", k=2)
+            nc.tensor.matmul(
+                out=task_sums[c][:], lhsT=ident_f32[:], rhs=slices[:, r, :], start=(r == 0), stop=(r == LEFT - 1)
             )
-            share_out = sum_pool.tile([P, OUT_COLS], F32)
+
+        def finish(c):
+            share_sums = sum_pool.tile([P, OUT_COLS], F32)
             nc.vector.tensor_reduce(
-                out=share_out[:],
+                out=share_sums[:],
                 in_=share_quarters[c][:].rearrange("p e (w n) -> p n (e w)", w=GROUPS),
                 axis=LAST_AXIS,
                 op=ADD,
             )
-            one_over = inverse_sums[c]
-            task_view = task_out[:].rearrange("p t (i u) -> p t i u", u=UNITS)
+            one_over = gate_pool.tile([P, SOFTMAXES], F32)
+            nc.vector.reciprocal(out=one_over[:], in_=gate_sums[c][:])
+            task_out = sum_pool.tile([P, TASKS, TILES, UNITS], F32)
             nc.vector.tensor_tensor(
-                out=task_view,
-                in0=task_view,
+                out=task_out[:],
+                in0=task_sums[c][:].rearrange("p (t i u) -> p t i u", t=TASKS, i=TILES),
                 in1=one_over[:, 0 : TASKS * TILES]
                 .rearrange("p (t i) -> p t i", t=TASKS)
                 .unsqueeze(3)
                 .to_broadcast([P, TASKS, TILES, UNITS]),
                 op=MULT,
             )
-            share_view = share_out[:].rearrange("p (i u) -> p i u", u=UNITS)
+            share_out = sum_pool.tile([P, TILES, UNITS], F32)
             nc.vector.tensor_tensor(
-                out=share_view,
-                in0=share_view,
+                out=share_out[:],
+                in0=share_sums[:].rearrange("p (i u) -> p i u", u=UNITS),
                 in1=one_over[:, TASKS * TILES : SOFTMAXES].unsqueeze(2).to_broadcast([P, TILES, UNITS]),
                 op=MULT,
             )
             own_rows = slice(TILES * c, TILES * (c + 1))
-            nc.sync.dma_start(out=task_out_by_partition[:, :, own_rows, :], in_=task_view)
-            nc.sync.dma_start(out=share_out_by_partition[:, own_rows, :], in_=share_view)
+            nc.sync.dma_start(out=task_out_by_partition[:, :, own_rows, :], in_=task_out[:])
+            nc.sync.dma_start(out=share_out_by_partition[:, own_rows, :], in_=share_out[:])
 
         load_x(0)
         load_x(1)
+        gate_logits(0)
         for i in range(TILES):
             transpose_x(0, i)
-        softmax_gates(0)
+        for w in range(GROUPS):
+            exponentiate(0, w)
         quantise_x(0)
         run_experts(0, 0)
-        for c in range(CHUNKS):
-            more = c + 1 < CHUNKS
+        for c in range(CHUNKS + LAG):
             if c + 2 < CHUNKS:
                 load_x(c + 2)
-            if more:
-                softmax_gates(c + 1)
+            if c + 1 < CHUNKS:
+                gate_logits(c + 1)
             for w in range(GROUPS):
-                if w + 1 < GROUPS:
+                if c < CHUNKS and w + 1 < GROUPS:
                     run_experts(c, w + 1)
-                elif more:
+                elif c + 1 < CHUNKS:
                     quantise_x(c + 1)
                     run_experts(c + 1, 0)
-                if more and w < TILES:
-                    transpose_x(c + 1, w)
-                weigh_experts(c, w)
-            halve_twice(c)
-            if c > 0:
-                finish(c - 1)
-        finish(CHUNKS - 1)
+                if c >= LAG and w < LEFT:
+                    add_quarter(c - LAG, w)
+                if c + 1 < CHUNKS:
+                    exponentiate(c + 1, w)
+                    if w < TILES:
+                        transpose_x(c + 1, w)
+                if c < CHUNKS:
+                    weigh_experts(c, w)
+            if c >= LAG:
+                finish(c - LAG)
+            if c < CHUNKS:
+                halve_twice(c)

@@ -13,6 +13,7 @@ ADD = mybir.AluOpType.add
 MULT = mybir.AluOpType.mult
 MAX = mybir.AluOpType.max
 LAST_AXIS = mybir.AxisListType.X
+LAST_TWO_AXES = mybir.AxisListType.XY
 EXP = mybir.ActivationFunctionType.Exp
 RELU = mybir.ActivationFunctionType.Relu
 
@@ -34,7 +35,10 @@ TASK_COLS = TASKS * TILES * TASK_GATE
 GATE_COLS = TASK_COLS + TILES * SHARE_GATE
 SOFTMAXES = TASKS * TILES + TILES
 OUT_COLS = TILES * UNITS
+ORDER = (SHARED,) + tuple(range(TASKS))
+SHARE_SLOTS = GROUPS + 2
 LEFT = 4
+LOGIT_BATCH = 4
 LAG = 2
 
 FLOPS = 2 * ROWS * D * GROUPS * N
@@ -52,6 +56,16 @@ def tile_plelayer_pa_t_e_kernel(
         gate_pool = ctx.enter_context(tc.tile_pool(name="gate_pool", bufs=4))
         sum_pool = ctx.enter_context(tc.tile_pool(name="sum_pool", bufs=2))
         psum = ctx.enter_context(tc.psum_pool(name="psum", bufs=1))
+
+        x_by_partition = x.rearrange("(p a) k -> p a k", a=ROWS_PER_PARTITION)
+        x_rows = {}
+
+        def load_x(c):
+            rows = x_pool.tile([P, TILES, D], BF16)
+            nc.sync.dma_start(out=rows[:], in_=x_by_partition[:, TILES * c : TILES * (c + 1), :])
+            x_rows[c] = rows
+
+        load_x(0)
 
         ident_f32 = const.tile([P, P], F32)
         make_identity(nc, ident_f32[:])
@@ -88,7 +102,7 @@ def tile_plelayer_pa_t_e_kernel(
         nc.vector.memset(bias_rows[:], 0.0)
         nc.sync.dma_start(out=bias_rows[0:TASKS, :], in_=eb0.rearrange("t u e -> t (u e)"))
         nc.sync.dma_start(out=bias_rows[SHARED : SHARED + 1, :], in_=ebs0.rearrange("u e -> (u e)").unsqueeze(0))
-        bias_columns = psum.tile([P, P], BF16, tag="logits")
+        bias_columns = psum.tile([P, P], BF16, tag="shared_by_row")
         nc.tensor.transpose(out=bias_columns[:], in_=bias_rows[:], identity=ident_bf16[:])
         expert_bias = const.tile([P, GROUPS], F32)
         nc.vector.tensor_copy(out=expert_bias[:], in_=bias_columns[:, 0:GROUPS])
@@ -121,18 +135,25 @@ def tile_plelayer_pa_t_e_kernel(
             in_=sgate_pre.rearrange("(p c i) s -> p c (i s)", c=CHUNKS, i=TILES),
         )
 
-        x_by_partition = x.rearrange("(p a) k -> p a k", a=ROWS_PER_PARTITION)
+        bias_in_psum = psum.tile([P, GATE_COLS], F32, tag="task_sums")
+        nc.tensor.matmul(out=bias_in_psum[:], lhsT=ones_bf16[:], rhs=gate_bias[:], start=True, stop=True)
+        bias_everywhere = const.tile([P, GATE_COLS], F32)
+        nc.vector.tensor_copy(out=bias_everywhere[:], in_=bias_in_psum[:])
+        logits = const.tile([P, CHUNKS, GATE_COLS], F32)
+        for first in range(0, CHUNKS, LOGIT_BATCH):
+            nc.gpsimd.tensor_tensor(
+                out=logits[:, first : first + LOGIT_BATCH, :],
+                in0=gate_pre[:, first : first + LOGIT_BATCH, :],
+                in1=bias_everywhere[:].unsqueeze(1).to_broadcast([P, LOGIT_BATCH, GATE_COLS]),
+                op=ADD,
+            )
+
         task_out_by_partition = out_0.rearrange("t (p a) u -> p t a u", a=ROWS_PER_PARTITION)
         share_out_by_partition = out_1.rearrange("(p a) u -> p a u", a=ROWS_PER_PARTITION)
 
-        x_rows, grouped, x_codes, x_scales, hidden = {}, {}, {}, {}, {}
-        logits, minus_max, gates, gate_sums = {}, {}, {}, {}
-        task_products, share_products, task_quarters, share_quarters, task_sums = {}, {}, {}, {}, {}
-
-        def load_x(c):
-            rows = x_pool.tile([P, TILES, D], BF16)
-            nc.sync.dma_start(out=rows[:], in_=x_by_partition[:, TILES * c : TILES * (c + 1), :])
-            x_rows[c] = rows
+        grouped, x_codes, x_scales, hidden, shared_by_row = {}, {}, {}, {}, {}
+        minus_max, gates, gate_sums = {}, {}, {}
+        task_products, share_products, task_quarters, task_sums = {}, {}, {}, {}
 
         def transpose_x(c, i):
             if i == 0:
@@ -179,33 +200,25 @@ def tile_plelayer_pa_t_e_kernel(
             nc.scalar.activation(out=active[:], in_=z[:], func=RELU, bias=expert_bias[:, w : w + 1], scale=1.0)
             hidden[c, w] = active
 
-        def gate_logits(c):
-            with_bias = psum.tile([P, GATE_COLS], F32, tag="logits")
-            nc.tensor.matmul(out=with_bias[:], lhsT=ones_bf16[:], rhs=gate_bias[:], start=True, stop=False)
-            nc.tensor.matmul(out=with_bias[:], lhsT=ident_bf16[:], rhs=gate_pre[:, c, :], start=False, stop=True)
-            max_of_8 = gate_pool.tile([P, GATE_COLS // EXPERTS], F32)
-            nc.vector.tensor_reduce(
-                out=max_of_8[:], in_=with_bias[:].rearrange("p (a e) -> p a e", e=EXPERTS), axis=LAST_AXIS, op=MAX
-            )
+        def gate_maxima(c):
             negated = gate_pool.tile([P, SOFTMAXES], F32)
-            split = TASK_COLS // EXPERTS
             nc.vector.tensor_reduce(
                 out=negated[:, 0 : TASKS * TILES],
-                in_=max_of_8[:, 0:split].rearrange("p (a h) -> p a h", h=TASK_GATE // EXPERTS),
+                in_=logits[:, c, 0:TASK_COLS].rearrange("p (a s) -> p a s", s=TASK_GATE),
                 axis=LAST_AXIS,
                 op=MAX,
                 negate=True,
             )
             nc.vector.tensor_reduce(
                 out=negated[:, TASKS * TILES : SOFTMAXES],
-                in_=max_of_8[:, split:].rearrange("p (a h) -> p a h", h=SHARE_GATE // EXPERTS),
+                in_=logits[:, c, TASK_COLS:GATE_COLS].rearrange("p (a s) -> p a s", s=SHARE_GATE),
                 axis=LAST_AXIS,
                 op=MAX,
                 negate=True,
             )
             weights = gate_pool.tile([P, GATE_COLS], F32)
             sums = gate_pool.tile([P, SOFTMAXES], F32)
-            logits[c], minus_max[c], gates[c], gate_sums[c] = with_bias, negated, weights, sums
+            minus_max[c], gates[c], gate_sums[c] = negated, weights, sums
 
         def exponentiate(c, w):
             width = SHARE_GATE if w == SHARED else TASK_GATE
@@ -214,7 +227,7 @@ def tile_plelayer_pa_t_e_kernel(
                 first = TILES * TASK_GATE * w + width * i
                 nc.scalar.activation(
                     out=gates[c][:, first : first + width],
-                    in_=logits[c][:, first : first + width],
+                    in_=logits[:, c, first : first + width],
                     func=EXP,
                     bias=minus_max[c][:, a : a + 1],
                     scale=1.0,
@@ -223,50 +236,60 @@ def tile_plelayer_pa_t_e_kernel(
 
         def gate_entries(c, first_col, width, first_entry):
             by_tile = gates[c][:, first_col : first_col + TILES * width].rearrange("p (i s) -> p i s", s=width)
-            eight = by_tile[:, :, first_entry : first_entry + EXPERTS].rearrange("p i e -> p e i")
-            return eight.unsqueeze(3).to_broadcast([P, EXPERTS, TILES, UNITS])
+            return by_tile[:, :, first_entry : first_entry + EXPERTS]
 
-        def weigh_experts(c, w):
-            if w == 0:
+        def weigh_experts(c, j):
+            w = ORDER[j]
+            if j == 0:
                 for_tasks = sum_pool.tile([P, EXPERTS, 2, TASKS, OUT_COLS], F32)
-                for_share = sum_pool.tile([P, EXPERTS, GROUPS, OUT_COLS], F32)
-                task_products[c] = for_tasks
-                share_products[c] = for_share
-            by_row = psum.tile([P, TILES, N], F32, tag="by_row", bufs=2)
+                for_share = sum_pool.tile([P, SHARE_SLOTS, TILES * N], F32, bufs=LAG + 1)
+                task_products[c], share_products[c] = for_tasks, for_share
+            if w == SHARED:
+                by_row = psum.tile([P, TILES, N], F32, tag="shared_by_row")
+                shared_by_row[c] = by_row
+            else:
+                by_row = psum.tile([P, TILES, N], F32, tag="task_by_row", bufs=2)
             for i in range(TILES):
                 nc.tensor.transpose(
                     out=by_row[:, i, :], in_=hidden[c, w][:, P * i : P * (i + 1)], identity=expert_major[:]
                 )
-            units = by_row[:].rearrange("p i (e u) -> p e i u", e=EXPERTS)
 
-            def product(out, gate):
+            def for_task(own_or_shared, experts_by_row):
+                entries = gate_entries(c, TILES * TASK_GATE * w, TASK_GATE, EXPERTS * own_or_shared)
                 nc.vector.tensor_tensor(
-                    out=out.rearrange("p e (i u) -> p e i u", u=UNITS), in0=units, in1=gate, op=MULT
+                    out=task_products[c][:, :, own_or_shared, w, :].rearrange("p e (i u) -> p e i u", u=UNITS),
+                    in0=experts_by_row[:].rearrange("p i (e u) -> p e i u", e=EXPERTS),
+                    in1=entries.rearrange("p i e -> p e i").unsqueeze(3).to_broadcast([P, EXPERTS, TILES, UNITS]),
+                    op=MULT,
                 )
 
-            task_width = TILES * TASK_GATE
-            if w == SHARED:
-                for t in range(TASKS):
-                    product(task_products[c][:, :, 1, t, :], gate_entries(c, task_width * t, TASK_GATE, EXPERTS))
-            else:
-                product(task_products[c][:, :, 0, w, :], gate_entries(c, task_width * w, TASK_GATE, 0))
-            product(share_products[c][:, :, w, :], gate_entries(c, TASK_COLS, SHARE_GATE, EXPERTS * w))
+            if w != SHARED:
+                for_task(0, by_row)
+                for_task(1, shared_by_row[c])
+            nc.vector.tensor_tensor(
+                out=share_products[c][:, j, :].rearrange("p (i u e) -> p i u e", i=TILES, e=EXPERTS),
+                in0=by_row[:].rearrange("p i (e u) -> p i u e", e=EXPERTS),
+                in1=gate_entries(c, TASK_COLS, SHARE_GATE, EXPERTS * w)
+                .unsqueeze(2)
+                .to_broadcast([P, TILES, UNITS, EXPERTS]),
+                op=MULT,
+            )
 
-        def halve_twice(c):
-            for products, quarters, name in (
-                (task_products[c][:].rearrange("p e k t n -> p e (k t n)"), task_quarters, "task"),
-                (share_products[c][:].rearrange("p e w n -> p e (w n)"), share_quarters, "share"),
-            ):
-                width = products.shape[2]
-                half = sum_pool.tile([P, EXPERTS // 2, width], F32, name=name + "_half")
-                nc.gpsimd.tensor_tensor(
-                    out=half[:], in0=products[:, 0 : EXPERTS // 2, :], in1=products[:, EXPERTS // 2 :, :], op=ADD
-                )
-                quarter = sum_pool.tile([P, EXPERTS // 4, width], F32, name=name + "_quarter")
-                nc.gpsimd.tensor_tensor(
-                    out=quarter[:], in0=half[:, 0 : EXPERTS // 4, :], in1=half[:, EXPERTS // 4 :, :], op=ADD
-                )
-                quarters[c] = quarter
+        def add_on_gpsimd(c):
+            products = task_products[c][:].rearrange("p e k t n -> p e (k t n)")
+            half = sum_pool.tile([P, EXPERTS // 2, 2 * TASKS * OUT_COLS], F32)
+            nc.gpsimd.tensor_tensor(
+                out=half[:], in0=products[:, 0 : EXPERTS // 2, :], in1=products[:, EXPERTS // 2 :, :], op=ADD
+            )
+            quarter = sum_pool.tile([P, EXPERTS // 4, 2 * TASKS * OUT_COLS], F32)
+            nc.gpsimd.tensor_tensor(
+                out=quarter[:], in0=half[:, 0 : EXPERTS // 4, :], in1=half[:, EXPERTS // 4 :, :], op=ADD
+            )
+            task_quarters[c] = quarter
+            share = share_products[c]
+            nc.gpsimd.tensor_tensor(
+                out=share[:, GROUPS:SHARE_SLOTS, :], in0=share[:, 0:4:2, :], in1=share[:, 1:4:2, :], op=ADD
+            )
 
         def add_quarter(c, r):
             if r == 0:
@@ -281,8 +304,8 @@ def tile_plelayer_pa_t_e_kernel(
             share_sums = sum_pool.tile([P, OUT_COLS], F32)
             nc.vector.tensor_reduce(
                 out=share_sums[:],
-                in_=share_quarters[c][:].rearrange("p e (w n) -> p n (e w)", w=GROUPS),
-                axis=LAST_AXIS,
+                in_=share_products[c][:, GROUPS - 1 : SHARE_SLOTS, :].rearrange("p s (n e) -> p n s e", e=EXPERTS),
+                axis=LAST_TWO_AXES,
                 op=ADD,
             )
             one_over = gate_pool.tile([P, SOFTMAXES], F32)
@@ -308,35 +331,34 @@ def tile_plelayer_pa_t_e_kernel(
             nc.sync.dma_start(out=task_out_by_partition[:, :, own_rows, :], in_=task_out[:])
             nc.sync.dma_start(out=share_out_by_partition[:, own_rows, :], in_=share_out[:])
 
-        load_x(0)
         load_x(1)
-        gate_logits(0)
+        gate_maxima(0)
         for i in range(TILES):
             transpose_x(0, i)
         for w in range(GROUPS):
             exponentiate(0, w)
         quantise_x(0)
-        run_experts(0, 0)
+        run_experts(0, ORDER[0])
         for c in range(CHUNKS + LAG):
             if c + 2 < CHUNKS:
                 load_x(c + 2)
             if c + 1 < CHUNKS:
-                gate_logits(c + 1)
-            for w in range(GROUPS):
-                if c < CHUNKS and w + 1 < GROUPS:
-                    run_experts(c, w + 1)
+                gate_maxima(c + 1)
+            for j in range(GROUPS):
+                if c < CHUNKS and j + 1 < GROUPS:
+                    run_experts(c, ORDER[j + 1])
                 elif c + 1 < CHUNKS:
                     quantise_x(c + 1)
-                    run_experts(c + 1, 0)
-                if c >= LAG and w < LEFT:
-                    add_quarter(c - LAG, w)
+                    run_experts(c + 1, ORDER[0])
+                if c >= LAG and j < LEFT:
+                    add_quarter(c - LAG, j)
                 if c + 1 < CHUNKS:
-                    exponentiate(c + 1, w)
-                    if w < TILES:
-                        transpose_x(c + 1, w)
+                    exponentiate(c + 1, j)
+                    if j < TILES:
+                        transpose_x(c + 1, j)
                 if c < CHUNKS:
-                    weigh_experts(c, w)
+                    weigh_experts(c, j)
             if c >= LAG:
                 finish(c - LAG)
             if c < CHUNKS:
-                halve_twice(c)
+                add_on_gpsimd(c)

@@ -16,6 +16,7 @@ LAST_AXIS = mybir.AxisListType.X
 LAST_TWO_AXES = mybir.AxisListType.XY
 EXP = mybir.ActivationFunctionType.Exp
 RELU = mybir.ActivationFunctionType.Relu
+COPY = mybir.ActivationFunctionType.Copy
 
 P = 128
 TASKS, ROWS, D, UNITS, EXPERTS = 4, 8192, 1024, 16, 8
@@ -38,7 +39,7 @@ OUT_COLS = TILES * UNITS
 ORDER = (SHARED,) + tuple(range(TASKS))
 SHARE_SLOTS = GROUPS + 2
 LEFT = 4
-LOGIT_BATCH = 4
+LOGIT_BATCH = 2
 LAG = 2
 
 FLOPS = 2 * ROWS * D * GROUPS * N
@@ -79,37 +80,30 @@ def tile_plelayer_pa_t_e_kernel(
             in_=ident_f32[:].rearrange("p (u e) -> p e u", e=EXPERTS),
         )
 
-        w_codes = const.tile([P, PASSES, GROUPS, N], U32, align_bytes=64)
-        task_words = ew0_words.rearrange("(t g) p n b -> g p t (n b)", g=PASSES).bitcast(I32)
-        for g in range(PASSES):
-            nc.sync.dma_start(out=w_codes[:, g, 0:TASKS, :].bitcast(I32), in_=task_words[g])
+        w_codes = const.tile([P, GROUPS, PASSES, N], U32, align_bytes=64)
         nc.sync.dma_start(
-            out=w_codes[:, :, SHARED, :].bitcast(I32), in_=ews0_words.rearrange("g p n b -> p g (n b)").bitcast(I32)
+            out=w_codes[:, 0:TASKS, :, :].rearrange("p t g n -> p (t g) n").bitcast(I32),
+            in_=ew0_words.rearrange("a p n b -> p a (n b)").bitcast(I32),
         )
-        w_scales = const.tile([P, PASSES, GROUPS, N], U8, align_bytes=64)
+        nc.sync.dma_start(
+            out=w_codes[:, SHARED, :, :].bitcast(I32), in_=ews0_words.rearrange("g p n b -> p g (n b)").bitcast(I32)
+        )
+        w_scales = const.tile([P, GROUPS, PASSES, N], U8, align_bytes=64)
         w_scales_i32 = w_scales[:].bitcast(I32)
         nc.vector.memset(w_scales_i32, 0)
-        task_scales = ew0_scales.rearrange("(t g) q n -> g q t n", g=PASSES).bitcast(I32)
+        task_scales = ew0_scales.rearrange("a q n -> q a n").bitcast(I32)
         shared_scales = ews0_scales.rearrange("g q n -> q g n").bitcast(I32)
         for quadrant in range(4):
             live = slice(32 * quadrant, 32 * quadrant + 4)
             rows = slice(4 * quadrant, 4 * quadrant + 4)
-            for g in range(PASSES):
-                nc.sync.dma_start(out=w_scales_i32[live, g, 0:TASKS, :], in_=task_scales[g, rows])
-            nc.sync.dma_start(out=w_scales_i32[live, :, SHARED, :], in_=shared_scales[rows])
-
-        bias_rows = const.tile([P, P], BF16)
-        nc.vector.memset(bias_rows[:], 0.0)
-        nc.sync.dma_start(out=bias_rows[0:TASKS, :], in_=eb0.rearrange("t u e -> t (u e)"))
-        nc.sync.dma_start(out=bias_rows[SHARED : SHARED + 1, :], in_=ebs0.rearrange("u e -> (u e)").unsqueeze(0))
-        bias_columns = psum.tile([P, P], BF16, tag="shared_by_row")
-        nc.tensor.transpose(out=bias_columns[:], in_=bias_rows[:], identity=ident_bf16[:])
-        expert_bias = const.tile([P, GROUPS], F32)
-        nc.vector.tensor_copy(out=expert_bias[:], in_=bias_columns[:, 0:GROUPS])
+            nc.sync.dma_start(
+                out=w_scales_i32[live, 0:TASKS, :, :].rearrange("p t g n -> p (t g) n"), in_=task_scales[rows]
+            )
+            nc.sync.dma_start(out=w_scales_i32[live, SHARED, :, :], in_=shared_scales[rows])
 
         bias_once = const.tile([1, TASKS * TASK_GATE + SHARE_GATE], BF16)
-        nc.sync.dma_start(out=bias_once[:, 0 : TASKS * TASK_GATE], in_=gb0.rearrange("t s -> (t s)").unsqueeze(0))
-        nc.sync.dma_start(out=bias_once[:, TASKS * TASK_GATE :], in_=gbs.unsqueeze(0))
+        nc.scalar.dma_start(out=bias_once[:, 0 : TASKS * TASK_GATE], in_=gb0.rearrange("t s -> (t s)").unsqueeze(0))
+        nc.scalar.dma_start(out=bias_once[:, TASKS * TASK_GATE :], in_=gbs.unsqueeze(0))
         gate_bias = const.tile([P, GATE_COLS], BF16)
         nc.vector.memset(gate_bias[:], 0.0)
         nc.vector.tensor_copy(
@@ -126,14 +120,23 @@ def tile_plelayer_pa_t_e_kernel(
 
         gate_pre = const.tile([P, CHUNKS, GATE_COLS], BF16)
         for t in range(TASKS):
-            nc.sync.dma_start(
+            nc.scalar.dma_start(
                 out=gate_pre[:, :, TILES * TASK_GATE * t : TILES * TASK_GATE * (t + 1)],
                 in_=gate_pre0[t].rearrange("(p c i) s -> p c (i s)", c=CHUNKS, i=TILES),
             )
-        nc.sync.dma_start(
+        nc.scalar.dma_start(
             out=gate_pre[:, :, TASK_COLS:GATE_COLS],
             in_=sgate_pre.rearrange("(p c i) s -> p c (i s)", c=CHUNKS, i=TILES),
         )
+
+        bias_rows = const.tile([P, P], BF16)
+        nc.vector.memset(bias_rows[:], 0.0)
+        nc.scalar.dma_start(out=bias_rows[0:TASKS, :], in_=eb0.rearrange("t u e -> t (u e)"))
+        nc.scalar.dma_start(out=bias_rows[SHARED : SHARED + 1, :], in_=ebs0.rearrange("u e -> (u e)").unsqueeze(0))
+        bias_columns = psum.tile([P, P], BF16, tag="shared_by_row")
+        nc.tensor.transpose(out=bias_columns[:], in_=bias_rows[:], identity=ident_bf16[:])
+        expert_bias = const.tile([P, GROUPS], F32)
+        nc.vector.tensor_copy(out=expert_bias[:], in_=bias_columns[:, 0:GROUPS])
 
         bias_in_psum = psum.tile([P, GATE_COLS], F32, tag="task_sums")
         nc.tensor.matmul(out=bias_in_psum[:], lhsT=ones_bf16[:], rhs=gate_bias[:], start=True, stop=True)
@@ -189,8 +192,8 @@ def tile_plelayer_pa_t_e_kernel(
                 columns = slice(CHUNK * g, CHUNK * (g + 1))
                 nc.tensor.matmul_mx(
                     out=z[:],
-                    lhsT=w_codes[:, g, w, :].bitcast(FP8X4),
-                    lhsT_scale=w_scales[:, g, w, :],
+                    lhsT=w_codes[:, w, g, :].bitcast(FP8X4),
+                    lhsT_scale=w_scales[:, w, g, :],
                     rhs=x_codes[c][:, columns].bitcast(FP8X4),
                     rhs_scale=x_scales[c][:, columns],
                     start=(g == 0),
@@ -310,26 +313,24 @@ def tile_plelayer_pa_t_e_kernel(
             )
             one_over = gate_pool.tile([P, SOFTMAXES], F32)
             nc.vector.reciprocal(out=one_over[:], in_=gate_sums[c][:])
-            task_out = sum_pool.tile([P, TASKS, TILES, UNITS], F32)
-            nc.vector.tensor_tensor(
-                out=task_out[:],
-                in0=task_sums[c][:].rearrange("p (t i u) -> p t i u", t=TASKS, i=TILES),
-                in1=one_over[:, 0 : TASKS * TILES]
-                .rearrange("p (t i) -> p t i", t=TASKS)
-                .unsqueeze(3)
-                .to_broadcast([P, TASKS, TILES, UNITS]),
-                op=MULT,
-            )
-            share_out = sum_pool.tile([P, TILES, UNITS], F32)
-            nc.vector.tensor_tensor(
-                out=share_out[:],
-                in0=share_sums[:].rearrange("p (i u) -> p i u", u=UNITS),
-                in1=one_over[:, TASKS * TILES : SOFTMAXES].unsqueeze(2).to_broadcast([P, TILES, UNITS]),
-                op=MULT,
-            )
+            task_out = sum_pool.tile([P, TASKS * OUT_COLS], F32)
+            share_out = sum_pool.tile([P, OUT_COLS], F32)
+            for a in range(SOFTMAXES):
+                if a < TASKS * TILES:
+                    units = slice(UNITS * a, UNITS * (a + 1))
+                    scaled, sums = task_out[:, units], task_sums[c][:, units]
+                else:
+                    units = slice(UNITS * (a - TASKS * TILES), UNITS * (a - TASKS * TILES + 1))
+                    scaled, sums = share_out[:, units], share_sums[:, units]
+                nc.scalar.activation(out=scaled, in_=sums, func=COPY, scale=one_over[:, a : a + 1])
             own_rows = slice(TILES * c, TILES * (c + 1))
-            nc.sync.dma_start(out=task_out_by_partition[:, :, own_rows, :], in_=task_out[:])
-            nc.sync.dma_start(out=share_out_by_partition[:, own_rows, :], in_=share_out[:])
+            nc.sync.dma_start(
+                out=task_out_by_partition[:, :, own_rows, :],
+                in_=task_out[:].rearrange("p (t i u) -> p t i u", t=TASKS, i=TILES),
+            )
+            nc.sync.dma_start(
+                out=share_out_by_partition[:, own_rows, :], in_=share_out[:].rearrange("p (i u) -> p i u", u=UNITS)
+            )
 
         load_x(1)
         gate_maxima(0)
@@ -339,6 +340,7 @@ def tile_plelayer_pa_t_e_kernel(
             exponentiate(0, w)
         quantise_x(0)
         run_experts(0, ORDER[0])
+        transpose_x(1, 0)
         for c in range(CHUNKS + LAG):
             if c + 2 < CHUNKS:
                 load_x(c + 2)
@@ -348,14 +350,17 @@ def tile_plelayer_pa_t_e_kernel(
                 if c < CHUNKS and j + 1 < GROUPS:
                     run_experts(c, ORDER[j + 1])
                 elif c + 1 < CHUNKS:
-                    quantise_x(c + 1)
                     run_experts(c + 1, ORDER[0])
                 if c >= LAG and j < LEFT:
                     add_quarter(c - LAG, j)
                 if c + 1 < CHUNKS:
                     exponentiate(c + 1, j)
-                    if j < TILES:
-                        transpose_x(c + 1, j)
+                if c + 1 < CHUNKS and j + 1 < TILES:
+                    transpose_x(c + 1, j + 1)
+                if c + 1 < CHUNKS and j + 1 == TILES:
+                    quantise_x(c + 1)
+                if c + 2 < CHUNKS and j == TILES:
+                    transpose_x(c + 2, 0)
                 if c < CHUNKS:
                     weigh_experts(c, j)
             if c >= LAG:

@@ -16,7 +16,6 @@ LAST_AXIS = mybir.AxisListType.X
 LAST_TWO_AXES = mybir.AxisListType.XY
 EXP = mybir.ActivationFunctionType.Exp
 RELU = mybir.ActivationFunctionType.Relu
-COPY = mybir.ActivationFunctionType.Copy
 
 P = 128
 TASKS, ROWS, D, UNITS, EXPERTS = 4, 8192, 1024, 16, 8
@@ -39,7 +38,8 @@ OUT_COLS = TILES * UNITS
 ORDER = (SHARED,) + tuple(range(TASKS))
 SHARE_SLOTS = GROUPS + 2
 LEFT = 4
-LOGIT_BATCH = 2
+LOGIT_BATCH = 4
+X_EARLY = 2
 LAG = 2
 
 FLOPS = 2 * ROWS * D * GROUPS * N
@@ -63,7 +63,8 @@ def tile_plelayer_pa_t_e_kernel(
 
         def load_x(c):
             rows = x_pool.tile([P, TILES, D], BF16)
-            nc.sync.dma_start(out=rows[:], in_=x_by_partition[:, TILES * c : TILES * (c + 1), :])
+            for i in range(TILES):
+                nc.sync.dma_start(out=rows[:, i, :], in_=x_by_partition[:, TILES * c + i, :])
             x_rows[c] = rows
 
         load_x(0)
@@ -80,30 +81,37 @@ def tile_plelayer_pa_t_e_kernel(
             in_=ident_f32[:].rearrange("p (u e) -> p e u", e=EXPERTS),
         )
 
-        w_codes = const.tile([P, GROUPS, PASSES, N], U32, align_bytes=64)
+        w_codes = const.tile([P, PASSES, GROUPS, N], U32, align_bytes=64)
+        task_words = ew0_words.rearrange("(t g) p n b -> g p t (n b)", g=PASSES).bitcast(I32)
+        for g in range(PASSES):
+            nc.sync.dma_start(out=w_codes[:, g, 0:TASKS, :].bitcast(I32), in_=task_words[g])
         nc.sync.dma_start(
-            out=w_codes[:, 0:TASKS, :, :].rearrange("p t g n -> p (t g) n").bitcast(I32),
-            in_=ew0_words.rearrange("a p n b -> p a (n b)").bitcast(I32),
+            out=w_codes[:, :, SHARED, :].bitcast(I32), in_=ews0_words.rearrange("g p n b -> p g (n b)").bitcast(I32)
         )
-        nc.sync.dma_start(
-            out=w_codes[:, SHARED, :, :].bitcast(I32), in_=ews0_words.rearrange("g p n b -> p g (n b)").bitcast(I32)
-        )
-        w_scales = const.tile([P, GROUPS, PASSES, N], U8, align_bytes=64)
+        w_scales = const.tile([P, PASSES, GROUPS, N], U8, align_bytes=64)
         w_scales_i32 = w_scales[:].bitcast(I32)
         nc.vector.memset(w_scales_i32, 0)
-        task_scales = ew0_scales.rearrange("a q n -> q a n").bitcast(I32)
+        task_scales = ew0_scales.rearrange("(t g) q n -> g q t n", g=PASSES).bitcast(I32)
         shared_scales = ews0_scales.rearrange("g q n -> q g n").bitcast(I32)
         for quadrant in range(4):
             live = slice(32 * quadrant, 32 * quadrant + 4)
             rows = slice(4 * quadrant, 4 * quadrant + 4)
-            nc.sync.dma_start(
-                out=w_scales_i32[live, 0:TASKS, :, :].rearrange("p t g n -> p (t g) n"), in_=task_scales[rows]
-            )
-            nc.sync.dma_start(out=w_scales_i32[live, SHARED, :, :], in_=shared_scales[rows])
+            for g in range(PASSES):
+                nc.sync.dma_start(out=w_scales_i32[live, g, 0:TASKS, :], in_=task_scales[g, rows])
+            nc.sync.dma_start(out=w_scales_i32[live, :, SHARED, :], in_=shared_scales[rows])
+
+        bias_rows = const.tile([P, P], BF16)
+        nc.vector.memset(bias_rows[:], 0.0)
+        nc.sync.dma_start(out=bias_rows[0:TASKS, :], in_=eb0.rearrange("t u e -> t (u e)"))
+        nc.sync.dma_start(out=bias_rows[SHARED : SHARED + 1, :], in_=ebs0.rearrange("u e -> (u e)").unsqueeze(0))
+        bias_columns = psum.tile([P, P], BF16, tag="shared_by_row")
+        nc.tensor.transpose(out=bias_columns[:], in_=bias_rows[:], identity=ident_bf16[:])
+        expert_bias = const.tile([P, GROUPS], F32)
+        nc.vector.tensor_copy(out=expert_bias[:], in_=bias_columns[:, 0:GROUPS])
 
         bias_once = const.tile([1, TASKS * TASK_GATE + SHARE_GATE], BF16)
-        nc.scalar.dma_start(out=bias_once[:, 0 : TASKS * TASK_GATE], in_=gb0.rearrange("t s -> (t s)").unsqueeze(0))
-        nc.scalar.dma_start(out=bias_once[:, TASKS * TASK_GATE :], in_=gbs.unsqueeze(0))
+        nc.sync.dma_start(out=bias_once[:, 0 : TASKS * TASK_GATE], in_=gb0.rearrange("t s -> (t s)").unsqueeze(0))
+        nc.sync.dma_start(out=bias_once[:, TASKS * TASK_GATE :], in_=gbs.unsqueeze(0))
         gate_bias = const.tile([P, GATE_COLS], BF16)
         nc.vector.memset(gate_bias[:], 0.0)
         nc.vector.tensor_copy(
@@ -120,23 +128,14 @@ def tile_plelayer_pa_t_e_kernel(
 
         gate_pre = const.tile([P, CHUNKS, GATE_COLS], BF16)
         for t in range(TASKS):
-            nc.scalar.dma_start(
+            nc.sync.dma_start(
                 out=gate_pre[:, :, TILES * TASK_GATE * t : TILES * TASK_GATE * (t + 1)],
                 in_=gate_pre0[t].rearrange("(p c i) s -> p c (i s)", c=CHUNKS, i=TILES),
             )
-        nc.scalar.dma_start(
+        nc.sync.dma_start(
             out=gate_pre[:, :, TASK_COLS:GATE_COLS],
             in_=sgate_pre.rearrange("(p c i) s -> p c (i s)", c=CHUNKS, i=TILES),
         )
-
-        bias_rows = const.tile([P, P], BF16)
-        nc.vector.memset(bias_rows[:], 0.0)
-        nc.scalar.dma_start(out=bias_rows[0:TASKS, :], in_=eb0.rearrange("t u e -> t (u e)"))
-        nc.scalar.dma_start(out=bias_rows[SHARED : SHARED + 1, :], in_=ebs0.rearrange("u e -> (u e)").unsqueeze(0))
-        bias_columns = psum.tile([P, P], BF16, tag="shared_by_row")
-        nc.tensor.transpose(out=bias_columns[:], in_=bias_rows[:], identity=ident_bf16[:])
-        expert_bias = const.tile([P, GROUPS], F32)
-        nc.vector.tensor_copy(out=expert_bias[:], in_=bias_columns[:, 0:GROUPS])
 
         bias_in_psum = psum.tile([P, GATE_COLS], F32, tag="task_sums")
         nc.tensor.matmul(out=bias_in_psum[:], lhsT=ones_bf16[:], rhs=gate_bias[:], start=True, stop=True)
@@ -155,7 +154,7 @@ def tile_plelayer_pa_t_e_kernel(
         share_out_by_partition = out_1.rearrange("(p a) u -> p a u", a=ROWS_PER_PARTITION)
 
         grouped, x_codes, x_scales, hidden, shared_by_row = {}, {}, {}, {}, {}
-        minus_max, gates, gate_sums = {}, {}, {}
+        minus_max, gates, gate_sums, inverse_sums = {}, {}, {}, {}
         task_products, share_products, task_quarters, task_sums = {}, {}, {}, {}
 
         def transpose_x(c, i):
@@ -192,8 +191,8 @@ def tile_plelayer_pa_t_e_kernel(
                 columns = slice(CHUNK * g, CHUNK * (g + 1))
                 nc.tensor.matmul_mx(
                     out=z[:],
-                    lhsT=w_codes[:, w, g, :].bitcast(FP8X4),
-                    lhsT_scale=w_scales[:, w, g, :],
+                    lhsT=w_codes[:, g, w, :].bitcast(FP8X4),
+                    lhsT_scale=w_scales[:, g, w, :],
                     rhs=x_codes[c][:, columns].bitcast(FP8X4),
                     rhs_scale=x_scales[c][:, columns],
                     start=(g == 0),
@@ -303,7 +302,12 @@ def tile_plelayer_pa_t_e_kernel(
                 out=task_sums[c][:], lhsT=ident_f32[:], rhs=slices[:, r, :], start=(r == 0), stop=(r == LEFT - 1)
             )
 
-        def finish(c):
+        def invert_gate_sums(c):
+            one_over = gate_pool.tile([P, SOFTMAXES], F32)
+            nc.vector.reciprocal(out=one_over[:], in_=gate_sums[c][:])
+            inverse_sums[c] = one_over
+
+        def finish_share(c):
             share_sums = sum_pool.tile([P, OUT_COLS], F32)
             nc.vector.tensor_reduce(
                 out=share_sums[:],
@@ -311,59 +315,68 @@ def tile_plelayer_pa_t_e_kernel(
                 axis=LAST_TWO_AXES,
                 op=ADD,
             )
-            one_over = gate_pool.tile([P, SOFTMAXES], F32)
-            nc.vector.reciprocal(out=one_over[:], in_=gate_sums[c][:])
-            task_out = sum_pool.tile([P, TASKS * OUT_COLS], F32)
-            share_out = sum_pool.tile([P, OUT_COLS], F32)
-            for a in range(SOFTMAXES):
-                if a < TASKS * TILES:
-                    units = slice(UNITS * a, UNITS * (a + 1))
-                    scaled, sums = task_out[:, units], task_sums[c][:, units]
-                else:
-                    units = slice(UNITS * (a - TASKS * TILES), UNITS * (a - TASKS * TILES + 1))
-                    scaled, sums = share_out[:, units], share_sums[:, units]
-                nc.scalar.activation(out=scaled, in_=sums, func=COPY, scale=one_over[:, a : a + 1])
-            own_rows = slice(TILES * c, TILES * (c + 1))
-            nc.sync.dma_start(
-                out=task_out_by_partition[:, :, own_rows, :],
-                in_=task_out[:].rearrange("p (t i u) -> p t i u", t=TASKS, i=TILES),
+            share_out = sum_pool.tile([P, TILES, UNITS], F32)
+            nc.vector.tensor_tensor(
+                out=share_out[:],
+                in0=share_sums[:].rearrange("p (i u) -> p i u", u=UNITS),
+                in1=inverse_sums[c][:, TASKS * TILES : SOFTMAXES].unsqueeze(2).to_broadcast([P, TILES, UNITS]),
+                op=MULT,
             )
-            nc.sync.dma_start(
-                out=share_out_by_partition[:, own_rows, :], in_=share_out[:].rearrange("p (i u) -> p i u", u=UNITS)
-            )
+            nc.sync.dma_start(out=share_out_by_partition[:, TILES * c : TILES * (c + 1), :], in_=share_out[:])
 
-        load_x(1)
-        gate_maxima(0)
-        for i in range(TILES):
-            transpose_x(0, i)
-        for w in range(GROUPS):
-            exponentiate(0, w)
-        quantise_x(0)
-        run_experts(0, ORDER[0])
-        transpose_x(1, 0)
-        for c in range(CHUNKS + LAG):
-            if c + 2 < CHUNKS:
-                load_x(c + 2)
-            if c + 1 < CHUNKS:
-                gate_maxima(c + 1)
-            for j in range(GROUPS):
-                if c < CHUNKS and j + 1 < GROUPS:
-                    run_experts(c, ORDER[j + 1])
-                elif c + 1 < CHUNKS:
-                    run_experts(c + 1, ORDER[0])
-                if c >= LAG and j < LEFT:
-                    add_quarter(c - LAG, j)
+        def finish_tasks(c):
+            task_out = sum_pool.tile([P, TASKS, TILES, UNITS], F32)
+            nc.vector.tensor_tensor(
+                out=task_out[:],
+                in0=task_sums[c][:].rearrange("p (t i u) -> p t i u", t=TASKS, i=TILES),
+                in1=inverse_sums[c][:, 0 : TASKS * TILES]
+                .rearrange("p (t i) -> p t i", t=TASKS)
+                .unsqueeze(3)
+                .to_broadcast([P, TASKS, TILES, UNITS]),
+                op=MULT,
+            )
+            nc.sync.dma_start(out=task_out_by_partition[:, :, TILES * c : TILES * (c + 1), :], in_=task_out[:])
+
+        with tc.manual_schedule():
+            load_x(1)
+            gate_maxima(0)
+            for i in range(TILES):
+                transpose_x(0, i)
+            for i in range(X_EARLY):
+                transpose_x(1, i)
+            for w in range(GROUPS):
+                exponentiate(0, w)
+            quantise_x(0)
+            run_experts(0, ORDER[0])
+            gate_maxima(1)
+            invert_gate_sums(0)
+            for c in range(CHUNKS + LAG):
+                late = c - LAG
+                if c + 2 < CHUNKS:
+                    load_x(c + 2)
+                for j in range(GROUPS):
+                    if c + 1 < CHUNKS and j == TILES - X_EARLY:
+                        quantise_x(c + 1)
+                    if c < CHUNKS and j + 1 < GROUPS:
+                        run_experts(c, ORDER[j + 1])
+                    elif c + 1 < CHUNKS:
+                        run_experts(c + 1, ORDER[0])
+                    if c < CHUNKS:
+                        weigh_experts(c, j)
+                    if c + 1 < CHUNKS and j + X_EARLY < TILES:
+                        transpose_x(c + 1, j + X_EARLY)
+                    if c + 2 < CHUNKS and j + X_EARLY >= GROUPS:
+                        transpose_x(c + 2, j + X_EARLY - GROUPS)
+                    if late >= 0 and j >= 1:
+                        add_quarter(late, j - 1)
+                    if c + 1 < CHUNKS:
+                        exponentiate(c + 1, j)
+                if late >= 0:
+                    finish_share(late)
+                    finish_tasks(late)
                 if c + 1 < CHUNKS:
-                    exponentiate(c + 1, j)
-                if c + 1 < CHUNKS and j + 1 < TILES:
-                    transpose_x(c + 1, j + 1)
-                if c + 1 < CHUNKS and j + 1 == TILES:
-                    quantise_x(c + 1)
-                if c + 2 < CHUNKS and j == TILES:
-                    transpose_x(c + 2, 0)
+                    invert_gate_sums(c + 1)
+                if c + 2 < CHUNKS:
+                    gate_maxima(c + 2)
                 if c < CHUNKS:
-                    weigh_experts(c, j)
-            if c >= LAG:
-                finish(c - LAG)
-            if c < CHUNKS:
-                add_on_gpsimd(c)
+                    add_on_gpsimd(c)

@@ -39,6 +39,7 @@ ORDER = (SHARED,) + tuple(range(TASKS))
 SHARE_SLOTS = GROUPS + 2
 LEFT = 4
 LOGIT_BATCH = 4
+X_AHEAD = 3
 X_EARLY = 2
 LAG = 2
 
@@ -51,7 +52,7 @@ def tile_plelayer_pa_t_e_kernel(
     nc = tc.nc
     with ExitStack() as ctx:
         const = ctx.enter_context(tc.tile_pool(name="const", bufs=1))
-        x_pool = ctx.enter_context(tc.tile_pool(name="x_pool", bufs=3))
+        x_pool = ctx.enter_context(tc.tile_pool(name="x_pool", bufs=X_AHEAD))
         mx_pool = ctx.enter_context(tc.tile_pool(name="mx_pool", bufs=2))
         hidden_pool = ctx.enter_context(tc.tile_pool(name="hidden_pool", bufs=3))
         gate_pool = ctx.enter_context(tc.tile_pool(name="gate_pool", bufs=4))
@@ -338,7 +339,8 @@ def tile_plelayer_pa_t_e_kernel(
             nc.sync.dma_start(out=task_out_by_partition[:, :, TILES * c : TILES * (c + 1), :], in_=task_out[:])
 
         with tc.manual_schedule():
-            load_x(1)
+            for c in range(1, X_AHEAD):
+                load_x(c)
             gate_maxima(0)
             for i in range(TILES):
                 transpose_x(0, i)
@@ -352,8 +354,8 @@ def tile_plelayer_pa_t_e_kernel(
             invert_gate_sums(0)
             for c in range(CHUNKS + LAG):
                 late = c - LAG
-                if c + 2 < CHUNKS:
-                    load_x(c + 2)
+                if c + X_AHEAD < CHUNKS:
+                    load_x(c + X_AHEAD)
                 for j in range(GROUPS):
                     if c + 1 < CHUNKS and j == TILES - X_EARLY:
                         quantise_x(c + 1)

@@ -36,11 +36,9 @@ GATE_COLS = TASK_COLS + TILES * SHARE_GATE
 SOFTMAXES = TASKS * TILES + TILES
 OUT_COLS = TILES * UNITS
 ORDER = (SHARED,) + tuple(range(TASKS))
-SHARE_SLOTS = GROUPS + 2
+SHARE_SLOTS = GROUPS + 1
 LEFT = 4
 LOGIT_BATCH = 4
-X_AHEAD = 3
-X_EARLY = 2
 LAG = 2
 
 FLOPS = 2 * ROWS * D * GROUPS * N
@@ -52,7 +50,7 @@ def tile_plelayer_pa_t_e_kernel(
     nc = tc.nc
     with ExitStack() as ctx:
         const = ctx.enter_context(tc.tile_pool(name="const", bufs=1))
-        x_pool = ctx.enter_context(tc.tile_pool(name="x_pool", bufs=X_AHEAD))
+        x_pool = ctx.enter_context(tc.tile_pool(name="x_pool", bufs=3))
         mx_pool = ctx.enter_context(tc.tile_pool(name="mx_pool", bufs=2))
         hidden_pool = ctx.enter_context(tc.tile_pool(name="hidden_pool", bufs=3))
         gate_pool = ctx.enter_context(tc.tile_pool(name="gate_pool", bufs=4))
@@ -64,8 +62,7 @@ def tile_plelayer_pa_t_e_kernel(
 
         def load_x(c):
             rows = x_pool.tile([P, TILES, D], BF16)
-            for i in range(TILES):
-                nc.sync.dma_start(out=rows[:, i, :], in_=x_by_partition[:, TILES * c + i, :])
+            nc.sync.dma_start(out=rows[:], in_=x_by_partition[:, TILES * c : TILES * (c + 1), :])
             x_rows[c] = rows
 
         load_x(0)
@@ -290,9 +287,7 @@ def tile_plelayer_pa_t_e_kernel(
             )
             task_quarters[c] = quarter
             share = share_products[c]
-            nc.gpsimd.tensor_tensor(
-                out=share[:, GROUPS:SHARE_SLOTS, :], in0=share[:, 0:4:2, :], in1=share[:, 1:4:2, :], op=ADD
-            )
+            nc.gpsimd.tensor_tensor(out=share[:, GROUPS, :], in0=share[:, 0, :], in1=share[:, 1, :], op=ADD)
 
         def add_quarter(c, r):
             if r == 0:
@@ -312,7 +307,7 @@ def tile_plelayer_pa_t_e_kernel(
             share_sums = sum_pool.tile([P, OUT_COLS], F32)
             nc.vector.tensor_reduce(
                 out=share_sums[:],
-                in_=share_products[c][:, GROUPS - 1 : SHARE_SLOTS, :].rearrange("p s (n e) -> p n s e", e=EXPERTS),
+                in_=share_products[c][:, 2:SHARE_SLOTS, :].rearrange("p s (n e) -> p n s e", e=EXPERTS),
                 axis=LAST_TWO_AXES,
                 op=ADD,
             )
@@ -338,47 +333,41 @@ def tile_plelayer_pa_t_e_kernel(
             )
             nc.sync.dma_start(out=task_out_by_partition[:, :, TILES * c : TILES * (c + 1), :], in_=task_out[:])
 
-        with tc.manual_schedule():
-            for c in range(1, X_AHEAD):
-                load_x(c)
-            gate_maxima(0)
-            for i in range(TILES):
-                transpose_x(0, i)
-            for i in range(X_EARLY):
-                transpose_x(1, i)
-            for w in range(GROUPS):
-                exponentiate(0, w)
-            quantise_x(0)
-            run_experts(0, ORDER[0])
-            gate_maxima(1)
-            invert_gate_sums(0)
-            for c in range(CHUNKS + LAG):
-                late = c - LAG
-                if c + X_AHEAD < CHUNKS:
-                    load_x(c + X_AHEAD)
-                for j in range(GROUPS):
-                    if c + 1 < CHUNKS and j == TILES - X_EARLY:
-                        quantise_x(c + 1)
-                    if c < CHUNKS and j + 1 < GROUPS:
-                        run_experts(c, ORDER[j + 1])
-                    elif c + 1 < CHUNKS:
-                        run_experts(c + 1, ORDER[0])
-                    if c < CHUNKS:
-                        weigh_experts(c, j)
-                    if c + 1 < CHUNKS and j + X_EARLY < TILES:
-                        transpose_x(c + 1, j + X_EARLY)
-                    if c + 2 < CHUNKS and j + X_EARLY >= GROUPS:
-                        transpose_x(c + 2, j + X_EARLY - GROUPS)
-                    if late >= 0 and j >= 1:
-                        add_quarter(late, j - 1)
-                    if c + 1 < CHUNKS:
-                        exponentiate(c + 1, j)
-                if late >= 0:
-                    finish_share(late)
-                    finish_tasks(late)
+        load_x(1)
+        gate_maxima(0)
+        for i in range(TILES):
+            transpose_x(0, i)
+        for w in range(GROUPS):
+            exponentiate(0, w)
+        quantise_x(0)
+        run_experts(0, ORDER[0])
+        transpose_x(1, 0)
+        for c in range(CHUNKS + LAG):
+            late = c - LAG
+            if c + 2 < CHUNKS:
+                load_x(c + 2)
+            if c + 1 < CHUNKS:
+                gate_maxima(c + 1)
+            for j in range(GROUPS):
+                if c < CHUNKS and j + 1 < GROUPS:
+                    run_experts(c, ORDER[j + 1])
+                elif c + 1 < CHUNKS:
+                    run_experts(c + 1, ORDER[0])
+                if late >= 0 and j < LEFT:
+                    add_quarter(late, j)
                 if c + 1 < CHUNKS:
-                    invert_gate_sums(c + 1)
-                if c + 2 < CHUNKS:
-                    gate_maxima(c + 2)
+                    exponentiate(c + 1, j)
+                if c + 1 < CHUNKS and j + 1 < TILES:
+                    transpose_x(c + 1, j + 1)
+                if c + 1 < CHUNKS and j + 1 == TILES:
+                    quantise_x(c + 1)
+                if c + 2 < CHUNKS and j == TILES:
+                    transpose_x(c + 2, 0)
                 if c < CHUNKS:
-                    add_on_gpsimd(c)
+                    weigh_experts(c, j)
+            if late >= 0:
+                invert_gate_sums(late)
+                finish_share(late)
+                finish_tasks(late)
+            if c < CHUNKS:
+                add_on_gpsimd(c)

@@ -16,6 +16,7 @@ LAST_AXIS = mybir.AxisListType.X
 LAST_TWO_AXES = mybir.AxisListType.XY
 EXP = mybir.ActivationFunctionType.Exp
 RELU = mybir.ActivationFunctionType.Relu
+COPY = mybir.ActivationFunctionType.Copy
 
 P = 128
 TASKS, ROWS, D, UNITS, EXPERTS = 4, 8192, 1024, 16, 8
@@ -36,7 +37,7 @@ GATE_COLS = TASK_COLS + TILES * SHARE_GATE
 SOFTMAXES = TASKS * TILES + TILES
 OUT_COLS = TILES * UNITS
 ORDER = (SHARED,) + tuple(range(TASKS))
-SHARE_SLOTS = GROUPS + 1
+SHARE_SLOTS = GROUPS + 2
 LEFT = 4
 LOGIT_BATCH = 4
 LAG = 2
@@ -152,7 +153,7 @@ def tile_plelayer_pa_t_e_kernel(
         share_out_by_partition = out_1.rearrange("(p a) u -> p a u", a=ROWS_PER_PARTITION)
 
         grouped, x_codes, x_scales, hidden, shared_by_row = {}, {}, {}, {}, {}
-        minus_max, gates, gate_sums, inverse_sums = {}, {}, {}, {}
+        minus_max, gates, gate_sums = {}, {}, {}
         task_products, share_products, task_quarters, task_sums = {}, {}, {}, {}
 
         def transpose_x(c, i):
@@ -287,7 +288,9 @@ def tile_plelayer_pa_t_e_kernel(
             )
             task_quarters[c] = quarter
             share = share_products[c]
-            nc.gpsimd.tensor_tensor(out=share[:, GROUPS, :], in0=share[:, 0, :], in1=share[:, 1, :], op=ADD)
+            nc.gpsimd.tensor_tensor(
+                out=share[:, GROUPS:SHARE_SLOTS, :], in0=share[:, 0:4:2, :], in1=share[:, 1:4:2, :], op=ADD
+            )
 
         def add_quarter(c, r):
             if r == 0:
@@ -298,40 +301,34 @@ def tile_plelayer_pa_t_e_kernel(
                 out=task_sums[c][:], lhsT=ident_f32[:], rhs=slices[:, r, :], start=(r == 0), stop=(r == LEFT - 1)
             )
 
-        def invert_gate_sums(c):
-            one_over = gate_pool.tile([P, SOFTMAXES], F32)
-            nc.vector.reciprocal(out=one_over[:], in_=gate_sums[c][:])
-            inverse_sums[c] = one_over
-
-        def finish_share(c):
+        def finish(c):
             share_sums = sum_pool.tile([P, OUT_COLS], F32)
             nc.vector.tensor_reduce(
                 out=share_sums[:],
-                in_=share_products[c][:, 2:SHARE_SLOTS, :].rearrange("p s (n e) -> p n s e", e=EXPERTS),
+                in_=share_products[c][:, GROUPS - 1 : SHARE_SLOTS, :].rearrange("p s (n e) -> p n s e", e=EXPERTS),
                 axis=LAST_TWO_AXES,
                 op=ADD,
             )
-            share_out = sum_pool.tile([P, TILES, UNITS], F32)
-            nc.vector.tensor_tensor(
-                out=share_out[:],
-                in0=share_sums[:].rearrange("p (i u) -> p i u", u=UNITS),
-                in1=inverse_sums[c][:, TASKS * TILES : SOFTMAXES].unsqueeze(2).to_broadcast([P, TILES, UNITS]),
-                op=MULT,
+            one_over = gate_pool.tile([P, SOFTMAXES], F32)
+            nc.vector.reciprocal(out=one_over[:], in_=gate_sums[c][:])
+            task_out = sum_pool.tile([P, TASKS * OUT_COLS], F32)
+            share_out = sum_pool.tile([P, OUT_COLS], F32)
+            for a in range(SOFTMAXES):
+                if a < TASKS * TILES:
+                    units = slice(UNITS * a, UNITS * (a + 1))
+                    scaled, sums = task_out[:, units], task_sums[c][:, units]
+                else:
+                    units = slice(UNITS * (a - TASKS * TILES), UNITS * (a - TASKS * TILES + 1))
+                    scaled, sums = share_out[:, units], share_sums[:, units]
+                nc.scalar.activation(out=scaled, in_=sums, func=COPY, scale=one_over[:, a : a + 1])
+            own_rows = slice(TILES * c, TILES * (c + 1))
+            nc.sync.dma_start(
+                out=task_out_by_partition[:, :, own_rows, :],
+                in_=task_out[:].rearrange("p (t i u) -> p t i u", t=TASKS, i=TILES),
             )
-            nc.sync.dma_start(out=share_out_by_partition[:, TILES * c : TILES * (c + 1), :], in_=share_out[:])
-
-        def finish_tasks(c):
-            task_out = sum_pool.tile([P, TASKS, TILES, UNITS], F32)
-            nc.vector.tensor_tensor(
-                out=task_out[:],
-                in0=task_sums[c][:].rearrange("p (t i u) -> p t i u", t=TASKS, i=TILES),
-                in1=inverse_sums[c][:, 0 : TASKS * TILES]
-                .rearrange("p (t i) -> p t i", t=TASKS)
-                .unsqueeze(3)
-                .to_broadcast([P, TASKS, TILES, UNITS]),
-                op=MULT,
+            nc.sync.dma_start(
+                out=share_out_by_partition[:, own_rows, :], in_=share_out[:].rearrange("p (i u) -> p i u", u=UNITS)
             )
-            nc.sync.dma_start(out=task_out_by_partition[:, :, TILES * c : TILES * (c + 1), :], in_=task_out[:])
 
         load_x(1)
         gate_maxima(0)
@@ -343,7 +340,6 @@ def tile_plelayer_pa_t_e_kernel(
         run_experts(0, ORDER[0])
         transpose_x(1, 0)
         for c in range(CHUNKS + LAG):
-            late = c - LAG
             if c + 2 < CHUNKS:
                 load_x(c + 2)
             if c + 1 < CHUNKS:
@@ -353,8 +349,8 @@ def tile_plelayer_pa_t_e_kernel(
                     run_experts(c, ORDER[j + 1])
                 elif c + 1 < CHUNKS:
                     run_experts(c + 1, ORDER[0])
-                if late >= 0 and j < LEFT:
-                    add_quarter(late, j)
+                if c >= LAG and j < LEFT:
+                    add_quarter(c - LAG, j)
                 if c + 1 < CHUNKS:
                     exponentiate(c + 1, j)
                 if c + 1 < CHUNKS and j + 1 < TILES:
@@ -365,9 +361,7 @@ def tile_plelayer_pa_t_e_kernel(
                     transpose_x(c + 2, 0)
                 if c < CHUNKS:
                     weigh_experts(c, j)
-            if late >= 0:
-                invert_gate_sums(late)
-                finish_share(late)
-                finish_tasks(late)
+            if c >= LAG:
+                finish(c - LAG)
             if c < CHUNKS:
                 add_on_gpsimd(c)

@@ -37,10 +37,10 @@ GATE_COLS = TASK_COLS + TILES * SHARE_GATE
 SOFTMAXES = TASKS * TILES + TILES
 OUT_COLS = TILES * UNITS
 ORDER = (SHARED,) + tuple(range(TASKS))
-SHARE_SLOTS = GROUPS + 2
 LEFT = 4
 LOGIT_BATCH = 4
 LAG = 2
+SUM_COLS = TASKS * OUT_COLS
 
 FLOPS = 2 * ROWS * D * GROUPS * N
 
@@ -51,10 +51,10 @@ def tile_plelayer_pa_t_e_kernel(
     nc = tc.nc
     with ExitStack() as ctx:
         const = ctx.enter_context(tc.tile_pool(name="const", bufs=1))
-        x_pool = ctx.enter_context(tc.tile_pool(name="x_pool", bufs=3))
-        mx_pool = ctx.enter_context(tc.tile_pool(name="mx_pool", bufs=2))
-        hidden_pool = ctx.enter_context(tc.tile_pool(name="hidden_pool", bufs=3))
-        gate_pool = ctx.enter_context(tc.tile_pool(name="gate_pool", bufs=4))
+        x_pool = ctx.enter_context(tc.tile_pool(name="x_pool", bufs=4))
+        mx_pool = ctx.enter_context(tc.tile_pool(name="mx_pool", bufs=3))
+        hidden_pool = ctx.enter_context(tc.tile_pool(name="hidden_pool", bufs=4))
+        gate_pool = ctx.enter_context(tc.tile_pool(name="gate_pool", bufs=6))
         sum_pool = ctx.enter_context(tc.tile_pool(name="sum_pool", bufs=2))
         psum = ctx.enter_context(tc.psum_pool(name="psum", bufs=1))
 
@@ -80,6 +80,9 @@ def tile_plelayer_pa_t_e_kernel(
             in_=ident_f32[:].rearrange("p (u e) -> p e u", e=EXPERTS),
         )
 
+        fold = const.tile([P, OUT_COLS], F32)
+        nc.vector.tensor_tensor(out=fold[:], in0=ident_f32[:, 0:OUT_COLS], in1=ident_f32[:, OUT_COLS:P], op=ADD)
+
         w_codes = const.tile([P, PASSES, GROUPS, N], U32, align_bytes=64)
         task_words = ew0_words.rearrange("(t g) p n b -> g p t (n b)", g=PASSES).bitcast(I32)
         for g in range(PASSES):
@@ -103,7 +106,7 @@ def tile_plelayer_pa_t_e_kernel(
         nc.vector.memset(bias_rows[:], 0.0)
         nc.sync.dma_start(out=bias_rows[0:TASKS, :], in_=eb0.rearrange("t u e -> t (u e)"))
         nc.sync.dma_start(out=bias_rows[SHARED : SHARED + 1, :], in_=ebs0.rearrange("u e -> (u e)").unsqueeze(0))
-        bias_columns = psum.tile([P, P], BF16, tag="shared_by_row")
+        bias_columns = psum.tile([P, P], BF16, tag="by_row", bufs=3)
         nc.tensor.transpose(out=bias_columns[:], in_=bias_rows[:], identity=ident_bf16[:])
         expert_bias = const.tile([P, GROUPS], F32)
         nc.vector.tensor_copy(out=expert_bias[:], in_=bias_columns[:, 0:GROUPS])
@@ -152,16 +155,16 @@ def tile_plelayer_pa_t_e_kernel(
         task_out_by_partition = out_0.rearrange("t (p a) u -> p t a u", a=ROWS_PER_PARTITION)
         share_out_by_partition = out_1.rearrange("(p a) u -> p a u", a=ROWS_PER_PARTITION)
 
-        grouped, x_codes, x_scales, hidden, shared_by_row = {}, {}, {}, {}, {}
+        grouped, x_codes, x_scales, hidden, experts_by_row = {}, {}, {}, {}, {}
         minus_max, gates, gate_sums = {}, {}, {}
-        task_products, share_products, task_quarters, task_sums = {}, {}, {}, {}
+        task_products, share_products, task_quarters, task_sums, share_sums = {}, {}, {}, {}, {}
 
         def transpose_x(c, i):
             if i == 0:
                 side_by_side = mx_pool.tile([P, PASSES * CHUNK * 4], BF16, align_bytes=64)
                 grouped[c] = side_by_side
             words = x_rows[c][:, i, :].bitcast(F32)
-            flipped = psum.tile([P, PASSES * WORD_PLANES, P], F32, tag="flipped", bufs=2)
+            flipped = psum.tile([P, PASSES * WORD_PLANES, P], F32, tag="flipped")
             for g in range(PASSES):
                 for h in range(WORD_PLANES):
                     first = (K_PASS // 2) * g + h
@@ -239,41 +242,44 @@ def tile_plelayer_pa_t_e_kernel(
             by_tile = gates[c][:, first_col : first_col + TILES * width].rearrange("p (i s) -> p i s", s=width)
             return by_tile[:, :, first_entry : first_entry + EXPERTS]
 
+        def rows_back(c, j):
+            by_row = psum.tile([P, TILES, N], F32, tag="by_row", bufs=3)
+            for i in range(TILES):
+                nc.tensor.transpose(
+                    out=by_row[:, i, :], in_=hidden[c, ORDER[j]][:, P * i : P * (i + 1)], identity=expert_major[:]
+                )
+            experts_by_row[c, j] = by_row
+
         def weigh_experts(c, j):
             w = ORDER[j]
             if j == 0:
                 for_tasks = sum_pool.tile([P, EXPERTS, 2, TASKS, OUT_COLS], F32)
-                for_share = sum_pool.tile([P, SHARE_SLOTS, TILES * N], F32, bufs=LAG + 1)
+                for_share = sum_pool.tile([P, GROUPS, TILES * N], F32, bufs=LAG + 1)
                 task_products[c], share_products[c] = for_tasks, for_share
-            if w == SHARED:
-                by_row = psum.tile([P, TILES, N], F32, tag="shared_by_row")
-                shared_by_row[c] = by_row
-            else:
-                by_row = psum.tile([P, TILES, N], F32, tag="task_by_row", bufs=2)
-            for i in range(TILES):
-                nc.tensor.transpose(
-                    out=by_row[:, i, :], in_=hidden[c, w][:, P * i : P * (i + 1)], identity=expert_major[:]
-                )
+            experts_first = experts_by_row[c, j][:].rearrange("p i (e u) -> p e i u", e=EXPERTS)
 
-            def for_task(own_or_shared, experts_by_row):
-                entries = gate_entries(c, TILES * TASK_GATE * w, TASK_GATE, EXPERTS * own_or_shared)
+            def multiply(out, entries):
                 nc.vector.tensor_tensor(
-                    out=task_products[c][:, :, own_or_shared, w, :].rearrange("p e (i u) -> p e i u", u=UNITS),
-                    in0=experts_by_row[:].rearrange("p i (e u) -> p e i u", e=EXPERTS),
+                    out=out.rearrange("p e (i u) -> p e i u", u=UNITS),
+                    in0=experts_first,
                     in1=entries.rearrange("p i e -> p e i").unsqueeze(3).to_broadcast([P, EXPERTS, TILES, UNITS]),
                     op=MULT,
                 )
 
-            if w != SHARED:
-                for_task(0, by_row)
-                for_task(1, shared_by_row[c])
-            nc.vector.tensor_tensor(
-                out=share_products[c][:, j, :].rearrange("p (i u e) -> p i u e", i=TILES, e=EXPERTS),
-                in0=by_row[:].rearrange("p i (e u) -> p i u e", e=EXPERTS),
-                in1=gate_entries(c, TASK_COLS, SHARE_GATE, EXPERTS * w)
-                .unsqueeze(2)
-                .to_broadcast([P, TILES, UNITS, EXPERTS]),
-                op=MULT,
+            def for_task(t, own_or_shared):
+                multiply(
+                    task_products[c][:, :, own_or_shared, t, :],
+                    gate_entries(c, TILES * TASK_GATE * t, TASK_GATE, EXPERTS * own_or_shared),
+                )
+
+            if w == SHARED:
+                for t in range(TASKS):
+                    for_task(t, 1)
+            else:
+                for_task(w, 0)
+            multiply(
+                share_products[c][:, j, :].rearrange("p (e n) -> p e n", e=EXPERTS),
+                gate_entries(c, TASK_COLS, SHARE_GATE, EXPERTS * w),
             )
 
         def add_on_gpsimd(c):
@@ -287,48 +293,80 @@ def tile_plelayer_pa_t_e_kernel(
                 out=quarter[:], in0=half[:, 0 : EXPERTS // 4, :], in1=half[:, EXPERTS // 4 :, :], op=ADD
             )
             task_quarters[c] = quarter
-            share = share_products[c]
-            nc.gpsimd.tensor_tensor(
-                out=share[:, GROUPS:SHARE_SLOTS, :], in0=share[:, 0:4:2, :], in1=share[:, 1:4:2, :], op=ADD
-            )
 
         def add_quarter(c, r):
             if r == 0:
-                totals = psum.tile([P, TASKS * OUT_COLS], F32, tag="task_sums")
+                totals = psum.tile([P, SUM_COLS], F32, tag="task_sums")
                 task_sums[c] = totals
             slices = task_quarters[c][:].rearrange("p e (k n) -> p (e k) n", k=2)
             nc.tensor.matmul(
                 out=task_sums[c][:], lhsT=ident_f32[:], rhs=slices[:, r, :], start=(r == 0), stop=(r == LEFT - 1)
             )
 
+        def add_share_blocks(c):
+            sums = psum.tile([P, P + OUT_COLS], F32, tag="share_sums")
+            share_sums[c] = sums
+            blocks = share_products[c][:].rearrange("p s (b m) -> p (s b) m", m=P)
+            count = GROUPS * TILES * N // P
+            for b in range(count):
+                nc.tensor.matmul(
+                    out=sums[:, 0:P], lhsT=blocks[:, b, :], rhs=ident_f32[:], is_transpose=True,
+                    start=(b == 0), stop=(b == count - 1),
+                )
+
+        def share_back(c):
+            in_sbuf = sum_pool.tile([P, P], F32)
+            nc.scalar.copy(out=in_sbuf[:], in_=share_sums[c][:, 0:P])
+            nc.tensor.matmul(out=share_sums[c][:, P:], lhsT=in_sbuf[:], rhs=fold[:], start=True, stop=True)
+
         def finish(c):
-            share_sums = sum_pool.tile([P, OUT_COLS], F32)
-            nc.vector.tensor_reduce(
-                out=share_sums[:],
-                in_=share_products[c][:, GROUPS - 1 : SHARE_SLOTS, :].rearrange("p s (n e) -> p n s e", e=EXPERTS),
-                axis=LAST_TWO_AXES,
-                op=ADD,
-            )
             one_over = gate_pool.tile([P, SOFTMAXES], F32)
             nc.vector.reciprocal(out=one_over[:], in_=gate_sums[c][:])
-            task_out = sum_pool.tile([P, TASKS * OUT_COLS], F32)
-            share_out = sum_pool.tile([P, OUT_COLS], F32)
-            for a in range(SOFTMAXES):
-                if a < TASKS * TILES:
-                    units = slice(UNITS * a, UNITS * (a + 1))
-                    scaled, sums = task_out[:, units], task_sums[c][:, units]
-                else:
-                    units = slice(UNITS * (a - TASKS * TILES), UNITS * (a - TASKS * TILES + 1))
-                    scaled, sums = share_out[:, units], share_sums[:, units]
-                nc.scalar.activation(out=scaled, in_=sums, func=COPY, scale=one_over[:, a : a + 1])
+            outputs = sum_pool.tile([P, SUM_COLS + OUT_COLS], F32)
+            nc.vector.tensor_tensor(
+                out=outputs[:, 0:SUM_COLS].rearrange("p (a u) -> p a u", u=UNITS),
+                in0=task_sums[c][:].rearrange("p (a u) -> p a u", u=UNITS),
+                in1=one_over[:, 0 : TASKS * TILES].unsqueeze(2).to_broadcast([P, TASKS * TILES, UNITS]),
+                op=MULT,
+            )
+            nc.vector.tensor_tensor(
+                out=outputs[:, SUM_COLS:].rearrange("p (a u) -> p a u", u=UNITS),
+                in0=share_sums[c][:, P:].rearrange("p (a u) -> p a u", u=UNITS),
+                in1=one_over[:, TASKS * TILES :].unsqueeze(2).to_broadcast([P, TILES, UNITS]),
+                op=MULT,
+            )
             own_rows = slice(TILES * c, TILES * (c + 1))
             nc.sync.dma_start(
                 out=task_out_by_partition[:, :, own_rows, :],
-                in_=task_out[:].rearrange("p (t i u) -> p t i u", t=TASKS, i=TILES),
+                in_=outputs[:, 0:SUM_COLS].rearrange("p (t i u) -> p t i u", t=TASKS, i=TILES),
             )
             nc.sync.dma_start(
-                out=share_out_by_partition[:, own_rows, :], in_=share_out[:].rearrange("p (i u) -> p i u", u=UNITS)
+                out=share_out_by_partition[:, own_rows, :],
+                in_=outputs[:, SUM_COLS:].rearrange("p (i u) -> p i u", u=UNITS),
             )
+
+        STEPS = CHUNKS * GROUPS
+
+        def feed(n):
+            if n < STEPS:
+                run_experts(n // GROUPS, ORDER[n % GROUPS])
+
+        def prepare(n):
+            c, phase = (n + 7) // GROUPS, (n + 7) % GROUPS
+            if c >= CHUNKS:
+                return
+            if phase < TILES:
+                transpose_x(c, phase)
+            else:
+                quantise_x(c)
+
+        def prepare_gates(n):
+            c, w = (n + 6) // GROUPS, (n + 6) % GROUPS
+            if c >= CHUNKS:
+                return
+            if w == 0:
+                gate_maxima(c)
+            exponentiate(c, w)
 
         load_x(1)
         gate_maxima(0)
@@ -337,31 +375,31 @@ def tile_plelayer_pa_t_e_kernel(
         for w in range(GROUPS):
             exponentiate(0, w)
         quantise_x(0)
-        run_experts(0, ORDER[0])
-        transpose_x(1, 0)
-        for c in range(CHUNKS + LAG):
-            if c + 2 < CHUNKS:
-                load_x(c + 2)
-            if c + 1 < CHUNKS:
-                gate_maxima(c + 1)
-            for j in range(GROUPS):
-                if c < CHUNKS and j + 1 < GROUPS:
-                    run_experts(c, ORDER[j + 1])
-                elif c + 1 < CHUNKS:
-                    run_experts(c + 1, ORDER[0])
-                if c >= LAG and j < LEFT:
-                    add_quarter(c - LAG, j)
-                if c + 1 < CHUNKS:
-                    exponentiate(c + 1, j)
-                if c + 1 < CHUNKS and j + 1 < TILES:
-                    transpose_x(c + 1, j + 1)
-                if c + 1 < CHUNKS and j + 1 == TILES:
-                    quantise_x(c + 1)
-                if c + 2 < CHUNKS and j == TILES:
-                    transpose_x(c + 2, 0)
-                if c < CHUNKS:
-                    weigh_experts(c, j)
-            if c >= LAG:
+        feed(0)
+        load_x(2)
+        for n in (-2, -1):
+            prepare(n)
+        feed(1)
+        prepare_gates(-1)
+        rows_back(0, 0)
+        for n in range(STEPS + LAG * GROUPS):
+            c, j = n // GROUPS, n % GROUPS
+            if j == 0 and c + 3 < CHUNKS:
+                load_x(c + 3)
+            feed(n + 2)
+            if n + 1 < STEPS:
+                rows_back((n + 1) // GROUPS, (n + 1) % GROUPS)
+            if n < STEPS:
+                weigh_experts(c, j)
+                if j == GROUPS - 1:
+                    add_on_gpsimd(c)
+            prepare(n)
+            prepare_gates(n)
+            if c >= LAG and j < LEFT:
+                add_quarter(c - LAG, j)
+            if c >= LAG and j == 0:
+                add_share_blocks(c - LAG)
+            if c >= LAG and j == 2:
+                share_back(c - LAG)
+            if c >= LAG and j == GROUPS - 1:
                 finish(c - LAG)
-            if c < CHUNKS:
-                add_on_gpsimd(c)

@@ -38,8 +38,9 @@ SOFTMAXES = TASKS * TILES + TILES
 OUT_COLS = TILES * UNITS
 ORDER = (SHARED,) + tuple(range(TASKS))
 LEFT = 4
-LOGIT_BATCH = 4
+HEAD_ROWS = 2 * TILES
 LAG = 2
+PE_SLOTS = 3
 SUM_COLS = TASKS * OUT_COLS
 
 FLOPS = 2 * ROWS * D * GROUPS * N
@@ -61,12 +62,36 @@ def tile_plelayer_pa_t_e_kernel(
         x_by_partition = x.rearrange("(p a) k -> p a k", a=ROWS_PER_PARTITION)
         x_rows = {}
 
-        def load_x(c):
+        def load_x(c, pieces=1):
             rows = x_pool.tile([P, TILES, D], BF16)
-            nc.sync.dma_start(out=rows[:], in_=x_by_partition[:, TILES * c : TILES * (c + 1), :])
+            step = TILES // pieces
+            for i in range(0, TILES, step):
+                nc.sync.dma_start(out=rows[:, i : i + step, :], in_=x_by_partition[:, TILES * c + i : TILES * c + i + step, :])
             x_rows[c] = rows
 
-        load_x(0)
+        load_x(0, pieces=TILES)
+
+        bias_once = const.tile([1, TASKS * TASK_GATE + SHARE_GATE], BF16)
+        nc.sync.dma_start(out=bias_once[:, 0 : TASKS * TASK_GATE], in_=gb0.rearrange("t s -> (t s)").unsqueeze(0))
+        nc.sync.dma_start(out=bias_once[:, TASKS * TASK_GATE :], in_=gbs.unsqueeze(0))
+        task_gate_pre = const.tile([P, TASKS, ROWS_PER_PARTITION * TASK_GATE], BF16)
+        share_gate_pre = const.tile([P, ROWS_PER_PARTITION * SHARE_GATE], BF16)
+
+        def load_gates(first_row, last_row):
+            nc.sync.dma_start(
+                out=task_gate_pre[:, :, TASK_GATE * first_row : TASK_GATE * last_row],
+                in_=gate_pre0.rearrange("t (p a) s -> p t (a s)", a=ROWS_PER_PARTITION)[
+                    :, :, TASK_GATE * first_row : TASK_GATE * last_row
+                ],
+            )
+            nc.sync.dma_start(
+                out=share_gate_pre[:, SHARE_GATE * first_row : SHARE_GATE * last_row],
+                in_=sgate_pre.rearrange("(p a) s -> p (a s)", a=ROWS_PER_PARTITION)[
+                    :, SHARE_GATE * first_row : SHARE_GATE * last_row
+                ],
+            )
+
+        load_gates(0, HEAD_ROWS)
 
         ident_f32 = const.tile([P, P], F32)
         make_identity(nc, ident_f32[:])
@@ -83,24 +108,26 @@ def tile_plelayer_pa_t_e_kernel(
         fold = const.tile([P, OUT_COLS], F32)
         nc.vector.tensor_tensor(out=fold[:], in0=ident_f32[:, 0:OUT_COLS], in1=ident_f32[:, OUT_COLS:P], op=ADD)
 
-        w_codes = const.tile([P, PASSES, GROUPS, N], U32, align_bytes=64)
-        task_words = ew0_words.rearrange("(t g) p n b -> g p t (n b)", g=PASSES).bitcast(I32)
-        for g in range(PASSES):
-            nc.sync.dma_start(out=w_codes[:, g, 0:TASKS, :].bitcast(I32), in_=task_words[g])
+        w_codes = const.tile([P, GROUPS, PASSES, N], U32, align_bytes=64)
         nc.sync.dma_start(
-            out=w_codes[:, :, SHARED, :].bitcast(I32), in_=ews0_words.rearrange("g p n b -> p g (n b)").bitcast(I32)
+            out=w_codes[:, 0:TASKS, :, :].rearrange("p t g n -> p (t g) n").bitcast(I32),
+            in_=ew0_words.rearrange("a p n b -> p a (n b)").bitcast(I32),
         )
-        w_scales = const.tile([P, PASSES, GROUPS, N], U8, align_bytes=64)
+        nc.sync.dma_start(
+            out=w_codes[:, SHARED, :, :].bitcast(I32), in_=ews0_words.rearrange("g p n b -> p g (n b)").bitcast(I32)
+        )
+        w_scales = const.tile([P, GROUPS, PASSES, N], U8, align_bytes=64)
         w_scales_i32 = w_scales[:].bitcast(I32)
         nc.vector.memset(w_scales_i32, 0)
-        task_scales = ew0_scales.rearrange("(t g) q n -> g q t n", g=PASSES).bitcast(I32)
+        task_scales = ew0_scales.rearrange("a q n -> q a n").bitcast(I32)
         shared_scales = ews0_scales.rearrange("g q n -> q g n").bitcast(I32)
         for quadrant in range(4):
             live = slice(32 * quadrant, 32 * quadrant + 4)
             rows = slice(4 * quadrant, 4 * quadrant + 4)
-            for g in range(PASSES):
-                nc.sync.dma_start(out=w_scales_i32[live, g, 0:TASKS, :], in_=task_scales[g, rows])
-            nc.sync.dma_start(out=w_scales_i32[live, :, SHARED, :], in_=shared_scales[rows])
+            nc.sync.dma_start(
+                out=w_scales_i32[live, 0:TASKS, :, :].rearrange("p t g n -> p (t g) n"), in_=task_scales[rows]
+            )
+            nc.sync.dma_start(out=w_scales_i32[live, SHARED, :, :], in_=shared_scales[rows])
 
         bias_rows = const.tile([P, P], BF16)
         nc.vector.memset(bias_rows[:], 0.0)
@@ -111,9 +138,6 @@ def tile_plelayer_pa_t_e_kernel(
         expert_bias = const.tile([P, GROUPS], F32)
         nc.vector.tensor_copy(out=expert_bias[:], in_=bias_columns[:, 0:GROUPS])
 
-        bias_once = const.tile([1, TASKS * TASK_GATE + SHARE_GATE], BF16)
-        nc.sync.dma_start(out=bias_once[:, 0 : TASKS * TASK_GATE], in_=gb0.rearrange("t s -> (t s)").unsqueeze(0))
-        nc.sync.dma_start(out=bias_once[:, TASKS * TASK_GATE :], in_=gbs.unsqueeze(0))
         gate_bias = const.tile([P, GATE_COLS], BF16)
         nc.vector.memset(gate_bias[:], 0.0)
         nc.vector.tensor_copy(
@@ -128,27 +152,23 @@ def tile_plelayer_pa_t_e_kernel(
             in_=bias_once[:, TASKS * TASK_GATE :].unsqueeze(1).to_broadcast([1, TILES, SHARE_GATE]),
         )
 
-        gate_pre = const.tile([P, CHUNKS, GATE_COLS], BF16)
-        for t in range(TASKS):
-            nc.sync.dma_start(
-                out=gate_pre[:, :, TILES * TASK_GATE * t : TILES * TASK_GATE * (t + 1)],
-                in_=gate_pre0[t].rearrange("(p c i) s -> p c (i s)", c=CHUNKS, i=TILES),
-            )
-        nc.sync.dma_start(
-            out=gate_pre[:, :, TASK_COLS:GATE_COLS],
-            in_=sgate_pre.rearrange("(p c i) s -> p c (i s)", c=CHUNKS, i=TILES),
-        )
-
         bias_in_psum = psum.tile([P, GATE_COLS], F32, tag="task_sums")
         nc.tensor.matmul(out=bias_in_psum[:], lhsT=ones_bf16[:], rhs=gate_bias[:], start=True, stop=True)
         bias_everywhere = const.tile([P, GATE_COLS], F32)
         nc.vector.tensor_copy(out=bias_everywhere[:], in_=bias_in_psum[:])
         logits = const.tile([P, CHUNKS, GATE_COLS], F32)
-        for first in range(0, CHUNKS, LOGIT_BATCH):
+
+        def add_gate_bias(c):
             nc.gpsimd.tensor_tensor(
-                out=logits[:, first : first + LOGIT_BATCH, :],
-                in0=gate_pre[:, first : first + LOGIT_BATCH, :],
-                in1=bias_everywhere[:].unsqueeze(1).to_broadcast([P, LOGIT_BATCH, GATE_COLS]),
+                out=logits[:, c, 0:TASK_COLS].rearrange("p (t n) -> p t n", t=TASKS),
+                in0=task_gate_pre[:, :, TILES * TASK_GATE * c : TILES * TASK_GATE * (c + 1)],
+                in1=bias_everywhere[:, 0:TASK_COLS].rearrange("p (t n) -> p t n", t=TASKS),
+                op=ADD,
+            )
+            nc.gpsimd.tensor_tensor(
+                out=logits[:, c, TASK_COLS:GATE_COLS],
+                in0=share_gate_pre[:, TILES * SHARE_GATE * c : TILES * SHARE_GATE * (c + 1)],
+                in1=bias_everywhere[:, TASK_COLS:GATE_COLS],
                 op=ADD,
             )
 
@@ -193,8 +213,8 @@ def tile_plelayer_pa_t_e_kernel(
                 columns = slice(CHUNK * g, CHUNK * (g + 1))
                 nc.tensor.matmul_mx(
                     out=z[:],
-                    lhsT=w_codes[:, g, w, :].bitcast(FP8X4),
-                    lhsT_scale=w_scales[:, g, w, :],
+                    lhsT=w_codes[:, w, g, :].bitcast(FP8X4),
+                    lhsT_scale=w_scales[:, w, g, :],
                     rhs=x_codes[c][:, columns].bitcast(FP8X4),
                     rhs_scale=x_scales[c][:, columns],
                     start=(g == 0),
@@ -277,10 +297,20 @@ def tile_plelayer_pa_t_e_kernel(
                     for_task(t, 1)
             else:
                 for_task(w, 0)
-            multiply(
-                share_products[c][:, j, :].rearrange("p (e n) -> p e n", e=EXPERTS),
-                gate_entries(c, TASK_COLS, SHARE_GATE, EXPERTS * w),
-            )
+            if j < PE_SLOTS:
+                multiply(
+                    share_products[c][:, j, :].rearrange("p (e n) -> p e n", e=EXPERTS),
+                    gate_entries(c, TASK_COLS, SHARE_GATE, EXPERTS * w),
+                )
+            else:
+                nc.vector.tensor_tensor(
+                    out=share_products[c][:, j, :].rearrange("p (i u e) -> p i u e", i=TILES, e=EXPERTS),
+                    in0=experts_by_row[c, j][:].rearrange("p i (e u) -> p i u e", e=EXPERTS),
+                    in1=gate_entries(c, TASK_COLS, SHARE_GATE, EXPERTS * w)
+                    .unsqueeze(2)
+                    .to_broadcast([P, TILES, UNITS, EXPERTS]),
+                    op=MULT,
+                )
 
         def add_on_gpsimd(c):
             products = task_products[c][:].rearrange("p e k t n -> p e (k t n)")
@@ -307,7 +337,7 @@ def tile_plelayer_pa_t_e_kernel(
             sums = psum.tile([P, P + OUT_COLS], F32, tag="share_sums")
             share_sums[c] = sums
             blocks = share_products[c][:].rearrange("p s (b m) -> p (s b) m", m=P)
-            count = GROUPS * TILES * N // P
+            count = PE_SLOTS * TILES * N // P
             for b in range(count):
                 nc.tensor.matmul(
                     out=sums[:, 0:P], lhsT=blocks[:, b, :], rhs=ident_f32[:], is_transpose=True,
@@ -329,12 +359,23 @@ def tile_plelayer_pa_t_e_kernel(
                 in1=one_over[:, 0 : TASKS * TILES].unsqueeze(2).to_broadcast([P, TASKS * TILES, UNITS]),
                 op=MULT,
             )
-            nc.vector.tensor_tensor(
-                out=outputs[:, SUM_COLS:].rearrange("p (a u) -> p a u", u=UNITS),
-                in0=share_sums[c][:, P:].rearrange("p (a u) -> p a u", u=UNITS),
-                in1=one_over[:, TASKS * TILES :].unsqueeze(2).to_broadcast([P, TILES, UNITS]),
-                op=MULT,
+            reduced = sum_pool.tile([P, OUT_COLS], F32)
+            nc.vector.tensor_reduce(
+                out=reduced[:],
+                in_=share_products[c][:, PE_SLOTS:GROUPS, :].rearrange("p s (n e) -> p n s e", e=EXPERTS),
+                axis=LAST_TWO_AXES,
+                op=ADD,
             )
+            both = sum_pool.tile([P, OUT_COLS], F32)
+            nc.vector.tensor_tensor(out=both[:], in0=share_sums[c][:, P:], in1=reduced[:], op=ADD)
+            for i in range(TILES):
+                units = slice(UNITS * i, UNITS * (i + 1))
+                nc.scalar.activation(
+                    out=outputs[:, SUM_COLS + UNITS * i : SUM_COLS + UNITS * (i + 1)],
+                    in_=both[:, units],
+                    func=COPY,
+                    scale=one_over[:, TASKS * TILES + i : TASKS * TILES + i + 1],
+                )
             own_rows = slice(TILES * c, TILES * (c + 1))
             nc.sync.dma_start(
                 out=task_out_by_partition[:, :, own_rows, :],
@@ -369,6 +410,9 @@ def tile_plelayer_pa_t_e_kernel(
             exponentiate(c, w)
 
         load_x(1)
+        load_gates(HEAD_ROWS, ROWS_PER_PARTITION)
+        add_gate_bias(0)
+        add_gate_bias(1)
         gate_maxima(0)
         for i in range(TILES):
             transpose_x(0, i)
@@ -386,6 +430,8 @@ def tile_plelayer_pa_t_e_kernel(
             c, j = n // GROUPS, n % GROUPS
             if j == 0 and c + 3 < CHUNKS:
                 load_x(c + 3)
+            if j == 0 and c + 2 < CHUNKS:
+                add_gate_bias(c + 2)
             feed(n + 2)
             if n + 1 < STEPS:
                 rows_back((n + 1) // GROUPS, (n + 1) % GROUPS)

@@ -313,18 +313,21 @@ def tile_plelayer_pa_t_e_kernel(
                 )
 
         def add_on_gpsimd(c):
+            adder = nc.vector if c == CHUNKS - 1 else nc.gpsimd
             products = task_products[c][:].rearrange("p e k t n -> p e (k t n)")
             half = sum_pool.tile([P, EXPERTS // 2, 2 * TASKS * OUT_COLS], F32)
-            nc.gpsimd.tensor_tensor(
+            adder.tensor_tensor(
                 out=half[:], in0=products[:, 0 : EXPERTS // 2, :], in1=products[:, EXPERTS // 2 :, :], op=ADD
             )
             quarter = sum_pool.tile([P, EXPERTS // 4, 2 * TASKS * OUT_COLS], F32)
-            nc.gpsimd.tensor_tensor(
+            adder.tensor_tensor(
                 out=quarter[:], in0=half[:, 0 : EXPERTS // 4, :], in1=half[:, EXPERTS // 4 :, :], op=ADD
             )
             task_quarters[c] = quarter
 
         def add_quarter(c, r):
+            if c == CHUNKS - 1:
+                return
             if r == 0:
                 totals = psum.tile([P, SUM_COLS], F32, tag="task_sums")
                 task_sums[c] = totals
@@ -352,6 +355,15 @@ def tile_plelayer_pa_t_e_kernel(
         def finish(c):
             one_over = gate_pool.tile([P, SOFTMAXES], F32)
             nc.vector.reciprocal(out=one_over[:], in_=gate_sums[c][:])
+            if c == CHUNKS - 1:
+                last_sums = sum_pool.tile([P, SUM_COLS], F32)
+                nc.vector.tensor_reduce(
+                    out=last_sums[:],
+                    in_=task_quarters[c][:].rearrange("p e (k n) -> p n (e k)", k=2),
+                    axis=LAST_AXIS,
+                    op=ADD,
+                )
+                task_sums[c] = last_sums
             outputs = sum_pool.tile([P, SUM_COLS + OUT_COLS], F32)
             nc.vector.tensor_tensor(
                 out=outputs[:, 0:SUM_COLS].rearrange("p (a u) -> p a u", u=UNITS),

@@ -158,17 +158,25 @@ def tile_plelayer_pa_t_e_kernel(
         nc.vector.tensor_copy(out=bias_everywhere[:], in_=bias_in_psum[:])
         logits = const.tile([P, CHUNKS, GATE_COLS], F32)
 
-        def add_gate_bias(c):
+        def add_gate_bias(first, last):
+            count = last - first
             nc.gpsimd.tensor_tensor(
-                out=logits[:, c, 0:TASK_COLS].rearrange("p (t n) -> p t n", t=TASKS),
-                in0=task_gate_pre[:, :, TILES * TASK_GATE * c : TILES * TASK_GATE * (c + 1)],
-                in1=bias_everywhere[:, 0:TASK_COLS].rearrange("p (t n) -> p t n", t=TASKS),
+                out=logits[:, first:last, 0:TASK_COLS].rearrange("p c (t n) -> p t c n", t=TASKS),
+                in0=task_gate_pre[:, :, TILES * TASK_GATE * first : TILES * TASK_GATE * last].rearrange(
+                    "p t (c n) -> p t c n", c=count
+                ),
+                in1=bias_everywhere[:, 0:TASK_COLS]
+                .rearrange("p (t n) -> p t n", t=TASKS)
+                .unsqueeze(2)
+                .to_broadcast([P, TASKS, count, TILES * TASK_GATE]),
                 op=ADD,
             )
             nc.gpsimd.tensor_tensor(
-                out=logits[:, c, TASK_COLS:GATE_COLS],
-                in0=share_gate_pre[:, TILES * SHARE_GATE * c : TILES * SHARE_GATE * (c + 1)],
-                in1=bias_everywhere[:, TASK_COLS:GATE_COLS],
+                out=logits[:, first:last, TASK_COLS:GATE_COLS],
+                in0=share_gate_pre[:, TILES * SHARE_GATE * first : TILES * SHARE_GATE * last].rearrange(
+                    "p (c n) -> p c n", c=count
+                ),
+                in1=bias_everywhere[:, TASK_COLS:GATE_COLS].unsqueeze(1).to_broadcast([P, count, TILES * SHARE_GATE]),
                 op=ADD,
             )
 
@@ -423,8 +431,8 @@ def tile_plelayer_pa_t_e_kernel(
 
         load_x(1)
         load_gates(HEAD_ROWS, ROWS_PER_PARTITION)
-        add_gate_bias(0)
-        add_gate_bias(1)
+        for first, last in ((0, 2), (2, 6), (6, 11), (11, CHUNKS)):
+            add_gate_bias(first, last)
         gate_maxima(0)
         for i in range(TILES):
             transpose_x(0, i)
@@ -442,8 +450,6 @@ def tile_plelayer_pa_t_e_kernel(
             c, j = n // GROUPS, n % GROUPS
             if j == 0 and c + 3 < CHUNKS:
                 load_x(c + 3)
-            if j == 0 and c + 2 < CHUNKS:
-                add_gate_bias(c + 2)
             feed(n + 2)
             if n + 1 < STEPS:
                 rows_back((n + 1) // GROUPS, (n + 1) % GROUPS)

@@ -413,7 +413,7 @@ def tile_plelayer_pa_t_e_kernel(
                 run_experts(n // GROUPS, ORDER[n % GROUPS])
 
         def prepare(n):
-            c, phase = (n + 7) // GROUPS, (n + 7) % GROUPS
+            c, phase = (n + 11) // GROUPS, (n + 11) % GROUPS
             if c >= CHUNKS:
                 return
             if phase < TILES:
@@ -441,11 +441,11 @@ def tile_plelayer_pa_t_e_kernel(
         quantise_x(0)
         feed(0)
         load_x(2)
-        for n in (-2, -1):
-            prepare(n)
         feed(1)
         prepare_gates(-1)
         rows_back(0, 0)
+        for n in range(-6, 0):
+            prepare(n)
         for n in range(STEPS + LAG * GROUPS):
             c, j = n // GROUPS, n % GROUPS
             if j == 0 and c + 3 < CHUNKS:

@@ -38,6 +38,7 @@ SOFTMAXES = TASKS * TILES + TILES
 OUT_COLS = TILES * UNITS
 ORDER = (SHARED,) + tuple(range(TASKS))
 LEFT = 4
+HEAD_BANKS = (("flipped", 1), ("z", 2), ("z", 2), ("by_row", 3))
 HEAD_ROWS = 2 * TILES
 LAG = 2
 PE_SLOTS = 3
@@ -72,8 +73,8 @@ def tile_plelayer_pa_t_e_kernel(
         load_x(0, pieces=TILES)
 
         bias_once = const.tile([1, TASKS * TASK_GATE + SHARE_GATE], BF16)
-        nc.sync.dma_start(out=bias_once[:, 0 : TASKS * TASK_GATE], in_=gb0.rearrange("t s -> (t s)").unsqueeze(0))
-        nc.sync.dma_start(out=bias_once[:, TASKS * TASK_GATE :], in_=gbs.unsqueeze(0))
+        nc.scalar.dma_start(out=bias_once[:, 0 : TASKS * TASK_GATE], in_=gb0.rearrange("t s -> (t s)").unsqueeze(0))
+        nc.scalar.dma_start(out=bias_once[:, TASKS * TASK_GATE :], in_=gbs.unsqueeze(0))
         task_gate_pre = const.tile([P, TASKS, ROWS_PER_PARTITION * TASK_GATE], BF16)
         share_gate_pre = const.tile([P, ROWS_PER_PARTITION * SHARE_GATE], BF16)
 
@@ -133,10 +134,12 @@ def tile_plelayer_pa_t_e_kernel(
         nc.vector.memset(bias_rows[:], 0.0)
         nc.sync.dma_start(out=bias_rows[0:TASKS, :], in_=eb0.rearrange("t u e -> t (u e)"))
         nc.sync.dma_start(out=bias_rows[SHARED : SHARED + 1, :], in_=ebs0.rearrange("u e -> (u e)").unsqueeze(0))
-        bias_columns = psum.tile([P, P], BF16, tag="by_row", bufs=3)
-        nc.tensor.transpose(out=bias_columns[:], in_=bias_rows[:], identity=ident_bf16[:])
         expert_bias = const.tile([P, GROUPS], F32)
-        nc.vector.tensor_copy(out=expert_bias[:], in_=bias_columns[:, 0:GROUPS])
+
+        def turn_expert_bias():
+            bias_columns = psum.tile([P, P], BF16, tag="by_row", bufs=3)
+            nc.tensor.transpose(out=bias_columns[:], in_=bias_rows[:], identity=ident_bf16[:])
+            nc.vector.tensor_copy(out=expert_bias[:], in_=bias_columns[:, 0:GROUPS])
 
         gate_bias = const.tile([P, GATE_COLS], BF16)
         nc.vector.memset(gate_bias[:], 0.0)
@@ -152,10 +155,13 @@ def tile_plelayer_pa_t_e_kernel(
             in_=bias_once[:, TASKS * TASK_GATE :].unsqueeze(1).to_broadcast([1, TILES, SHARE_GATE]),
         )
 
-        bias_in_psum = psum.tile([P, GATE_COLS], F32, tag="task_sums")
-        nc.tensor.matmul(out=bias_in_psum[:], lhsT=ones_bf16[:], rhs=gate_bias[:], start=True, stop=True)
         bias_everywhere = const.tile([P, GATE_COLS], F32)
-        nc.vector.tensor_copy(out=bias_everywhere[:], in_=bias_in_psum[:])
+
+        def spread_gate_bias():
+            bias_in_psum = psum.tile([P, GATE_COLS], F32, tag="task_sums")
+            nc.tensor.matmul(out=bias_in_psum[:], lhsT=ones_bf16[:], rhs=gate_bias[:], start=True, stop=True)
+            nc.vector.tensor_copy(out=bias_everywhere[:], in_=bias_in_psum[:])
+
         logits = const.tile([P, CHUNKS, GATE_COLS], F32)
 
         def add_gate_bias(first, last):
@@ -192,7 +198,8 @@ def tile_plelayer_pa_t_e_kernel(
                 side_by_side = mx_pool.tile([P, PASSES * CHUNK * 4], BF16, align_bytes=64)
                 grouped[c] = side_by_side
             words = x_rows[c][:, i, :].bitcast(F32)
-            flipped = psum.tile([P, PASSES * WORD_PLANES, P], F32, tag="flipped")
+            tag, bufs = HEAD_BANKS[i] if c == 0 else HEAD_BANKS[0]
+            flipped = psum.tile([P, PASSES * WORD_PLANES, P], F32, tag=tag, bufs=bufs)
             for g in range(PASSES):
                 for h in range(WORD_PLANES):
                     first = (K_PASS // 2) * g + h
@@ -208,10 +215,18 @@ def tile_plelayer_pa_t_e_kernel(
                 in_=flipped[:].rearrange("p (g h) n -> p g n h", h=WORD_PLANES),
             )
 
-        def quantise_x(c):
+        def quantise_x(c, pieces=1):
             codes = mx_pool.tile([P, PASSES * CHUNK], U32, align_bytes=64)
             scales = mx_pool.tile([P, PASSES * CHUNK], U8, align_bytes=64)
-            nc.vector.quantize_mx(out=codes[:].bitcast(FP8X4), scales=scales[:], in_=grouped[c][:])
+            width = PASSES * CHUNK if pieces == 1 else P
+            for first in range(0, CHUNK, CHUNK // pieces):
+                for g in range(1 if pieces == 1 else PASSES):
+                    columns = slice(CHUNK * g + first, CHUNK * g + first + width)
+                    nc.vector.quantize_mx(
+                        out=codes[:, columns].bitcast(FP8X4),
+                        scales=scales[:, columns],
+                        in_=grouped[c][:, 4 * columns.start : 4 * columns.stop],
+                    )
             x_codes[c] = codes
             x_scales[c] = scales
 
@@ -431,19 +446,24 @@ def tile_plelayer_pa_t_e_kernel(
 
         load_x(1)
         load_gates(HEAD_ROWS, ROWS_PER_PARTITION)
-        for first, last in ((0, 2), (2, 6), (6, 11), (11, CHUNKS)):
-            add_gate_bias(first, last)
+        load_x(2)
+        transpose_x(0, 0)
+        transpose_x(0, 1)
+        spread_gate_bias()
+        transpose_x(0, 2)
+        transpose_x(0, 3)
+        add_gate_bias(0, 1)
+        quantise_x(0, pieces=TILES)
         gate_maxima(0)
-        for i in range(TILES):
-            transpose_x(0, i)
+        turn_expert_bias()
+        feed(0)
         for w in range(GROUPS):
             exponentiate(0, w)
-        quantise_x(0)
-        feed(0)
-        load_x(2)
-        feed(1)
-        prepare_gates(-1)
         rows_back(0, 0)
+        feed(1)
+        for first, last in ((1, 4), (4, 9), (9, CHUNKS)):
+            add_gate_bias(first, last)
+        prepare_gates(-1)
         for n in range(-6, 0):
             prepare(n)
         for n in range(STEPS + LAG * GROUPS):

@@ -293,12 +293,18 @@ def tile_plelayer_pa_t_e_kernel(
                 )
             experts_by_row[c, j] = by_row
 
+        def last_task_slots(c):
+            return task_products[c][:].rearrange("p e k t n -> p (e k t n)").rearrange(
+                "p (k t e n) -> p k t e n", k=2, t=TASKS, e=EXPERTS
+            )
+
         def weigh_experts(c, j):
             w = ORDER[j]
             if j == 0:
                 for_tasks = sum_pool.tile([P, EXPERTS, 2, TASKS, OUT_COLS], F32)
                 for_share = sum_pool.tile([P, GROUPS, TILES * N], F32, bufs=LAG + 1)
                 task_products[c], share_products[c] = for_tasks, for_share
+            last = c == CHUNKS - 1
             experts_first = experts_by_row[c, j][:].rearrange("p i (e u) -> p e i u", e=EXPERTS)
 
             def multiply(out, entries):
@@ -310,8 +316,9 @@ def tile_plelayer_pa_t_e_kernel(
                 )
 
             def for_task(t, own_or_shared):
+                by_slot = last_task_slots(c)[:, own_or_shared, t, :, :] if last else task_products[c][:, :, own_or_shared, t, :]
                 multiply(
-                    task_products[c][:, :, own_or_shared, t, :],
+                    by_slot,
                     gate_entries(c, TILES * TASK_GATE * t, TASK_GATE, EXPERTS * own_or_shared),
                 )
 
@@ -320,7 +327,7 @@ def tile_plelayer_pa_t_e_kernel(
                     for_task(t, 1)
             else:
                 for_task(w, 0)
-            if j < PE_SLOTS:
+            if j < PE_SLOTS or last:
                 multiply(
                     share_products[c][:, j, :].rearrange("p (e n) -> p e n", e=EXPERTS),
                     gate_entries(c, TASK_COLS, SHARE_GATE, EXPERTS * w),
@@ -336,31 +343,40 @@ def tile_plelayer_pa_t_e_kernel(
                 )
 
         def add_on_gpsimd(c):
-            adder = nc.vector if c == CHUNKS - 1 else nc.gpsimd
             products = task_products[c][:].rearrange("p e k t n -> p e (k t n)")
             half = sum_pool.tile([P, EXPERTS // 2, 2 * TASKS * OUT_COLS], F32)
-            adder.tensor_tensor(
+            nc.gpsimd.tensor_tensor(
                 out=half[:], in0=products[:, 0 : EXPERTS // 2, :], in1=products[:, EXPERTS // 2 :, :], op=ADD
             )
             quarter = sum_pool.tile([P, EXPERTS // 4, 2 * TASKS * OUT_COLS], F32)
-            adder.tensor_tensor(
+            nc.gpsimd.tensor_tensor(
                 out=quarter[:], in0=half[:, 0 : EXPERTS // 4, :], in1=half[:, EXPERTS // 4 :, :], op=ADD
             )
             task_quarters[c] = quarter
 
-        def add_quarter(c, r):
-            if c == CHUNKS - 1:
-                return
-            if r == 0:
-                totals = psum.tile([P, SUM_COLS], F32, tag="task_sums")
+        def turn_tasks(c, half):
+            if half == 0:
+                totals = psum.tile([P, 2 * SUM_COLS], F32, tag="task_sums")
                 task_sums[c] = totals
-            slices = task_quarters[c][:].rearrange("p e (k n) -> p (e k) n", k=2)
-            nc.tensor.matmul(
-                out=task_sums[c][:], lhsT=ident_f32[:], rhs=slices[:, r, :], start=(r == 0), stop=(r == LEFT - 1)
-            )
+            blocks = task_quarters[c][:].rearrange("p e (k h m) -> p (e k) h m", k=2, m=P)
+            for r in range(LEFT):
+                nc.tensor.matmul(
+                    out=task_sums[c][:, P * half : P * (half + 1)], lhsT=blocks[:, r, half, :], rhs=ident_f32[:],
+                    is_transpose=True, start=(r == 0), stop=(r == LEFT - 1),
+                )
+
+        def tasks_back(c):
+            turned = sum_pool.tile([P, SUM_COLS], F32)
+            nc.scalar.copy(out=turned[:], in_=task_sums[c][:, 0:SUM_COLS])
+            for first in range(0, SUM_COLS, P):
+                nc.tensor.transpose(
+                    out=task_sums[c][:, SUM_COLS + first : SUM_COLS + first + P],
+                    in_=turned[:, first : first + P],
+                    identity=ident_f32[:],
+                )
 
         def add_share_blocks(c):
-            sums = psum.tile([P, P + OUT_COLS], F32, tag="share_sums")
+            sums = psum.tile([P, P + OUT_COLS], F32, tag="flipped" if c == CHUNKS - 3 else "share_sums")
             share_sums[c] = sums
             blocks = share_products[c][:].rearrange("p s (b m) -> p (s b) m", m=P)
             count = PE_SLOTS * TILES * N // P
@@ -378,19 +394,10 @@ def tile_plelayer_pa_t_e_kernel(
         def finish(c):
             one_over = gate_pool.tile([P, SOFTMAXES], F32)
             nc.vector.reciprocal(out=one_over[:], in_=gate_sums[c][:])
-            if c == CHUNKS - 1:
-                last_sums = sum_pool.tile([P, SUM_COLS], F32)
-                nc.vector.tensor_reduce(
-                    out=last_sums[:],
-                    in_=task_quarters[c][:].rearrange("p e (k n) -> p n (e k)", k=2),
-                    axis=LAST_AXIS,
-                    op=ADD,
-                )
-                task_sums[c] = last_sums
             outputs = sum_pool.tile([P, SUM_COLS + OUT_COLS], F32)
             nc.vector.tensor_tensor(
                 out=outputs[:, 0:SUM_COLS].rearrange("p (a u) -> p a u", u=UNITS),
-                in0=task_sums[c][:].rearrange("p (a u) -> p a u", u=UNITS),
+                in0=task_sums[c][:, SUM_COLS:].rearrange("p (a u) -> p a u", u=UNITS),
                 in1=one_over[:, 0 : TASKS * TILES].unsqueeze(2).to_broadcast([P, TASKS * TILES, UNITS]),
                 op=MULT,
             )
@@ -411,6 +418,9 @@ def tile_plelayer_pa_t_e_kernel(
                     func=COPY,
                     scale=one_over[:, TASKS * TILES + i : TASKS * TILES + i + 1],
                 )
+            store(c, outputs)
+
+        def store(c, outputs):
             own_rows = slice(TILES * c, TILES * (c + 1))
             nc.sync.dma_start(
                 out=task_out_by_partition[:, :, own_rows, :],
@@ -420,6 +430,59 @@ def tile_plelayer_pa_t_e_kernel(
                 out=share_out_by_partition[:, own_rows, :],
                 in_=outputs[:, SUM_COLS:].rearrange("p (i u) -> p i u", u=UNITS),
             )
+
+        last_sums_in_psum = {}
+
+        def add_blocks(out, products, first, last):
+            blocks = products.rearrange("p (b m) -> p b m", m=P)
+            for b in range(EXPERTS // 2):
+                nc.tensor.matmul(
+                    out=out, lhsT=blocks[:, b, :], rhs=ident_f32[:], is_transpose=True,
+                    start=(first and b == 0), stop=(last and b == EXPERTS // 2 - 1),
+                )
+
+        def add_last_task(t):
+            c = CHUNKS - 1
+            if t == 0:
+                by_task = psum.tile([P, TASKS, P], F32, tag="flipped")
+                last_sums_in_psum["tasks"] = by_task
+            for k in (1, 0):
+                add_blocks(
+                    last_sums_in_psum["tasks"][:, t, :],
+                    last_task_slots(c)[:, k, t, :, :].rearrange("p e n -> p (e n)"),
+                    first=(k == 1),
+                    last=(k == 0),
+                )
+
+        def add_last_share(j):
+            if j == 0:
+                by_share = psum.tile([P, P], F32, tag="z", bufs=2)
+                last_sums_in_psum["share"] = by_share
+            add_blocks(
+                last_sums_in_psum["share"][:], share_products[CHUNKS - 1][:, j, :], first=(j == 0), last=(j == GROUPS - 1)
+            )
+
+        def last_back(a):
+            if a == 0:
+                totals = psum.tile([P, GROUPS, OUT_COLS], F32, tag="z", bufs=2)
+                last_sums_in_psum["all"] = totals
+            in_sbuf = sum_pool.tile([P, P], F32)
+            source = last_sums_in_psum["share"][:] if a == SHARED else last_sums_in_psum["tasks"][:, a, :]
+            nc.scalar.copy(out=in_sbuf[:], in_=source)
+            nc.tensor.matmul(out=last_sums_in_psum["all"][:, a, :], lhsT=in_sbuf[:], rhs=fold[:], start=True, stop=True)
+
+        def finish_last():
+            c = CHUNKS - 1
+            one_over = gate_pool.tile([P, SOFTMAXES], F32)
+            nc.vector.reciprocal(out=one_over[:], in_=gate_sums[c][:])
+            outputs = sum_pool.tile([P, SUM_COLS + OUT_COLS], F32)
+            nc.vector.tensor_tensor(
+                out=outputs[:].rearrange("p (a u) -> p a u", u=UNITS),
+                in0=last_sums_in_psum["all"][:].rearrange("p a (i u) -> p (a i) u", u=UNITS),
+                in1=one_over[:].unsqueeze(2).to_broadcast([P, SOFTMAXES, UNITS]),
+                op=MULT,
+            )
+            store(c, outputs)
 
         STEPS = CHUNKS * GROUPS
 
@@ -466,24 +529,75 @@ def tile_plelayer_pa_t_e_kernel(
         prepare_gates(-1)
         for n in range(-6, 0):
             prepare(n)
-        for n in range(STEPS + LAG * GROUPS):
+        for n in range(STEPS):
             c, j = n // GROUPS, n % GROUPS
             if j == 0 and c + 3 < CHUNKS:
                 load_x(c + 3)
-            feed(n + 2)
+            if c < CHUNKS - 2:
+                feed(n + 2)
+            else:
+                if n == (CHUNKS - 2) * GROUPS:
+                    feed(n + 2)
+                feed(n + 3)
             if n + 1 < STEPS:
                 rows_back((n + 1) // GROUPS, (n + 1) % GROUPS)
-            if n < STEPS:
-                weigh_experts(c, j)
-                if j == GROUPS - 1:
-                    add_on_gpsimd(c)
+            weigh_experts(c, j)
+            if j == GROUPS - 1 and c < CHUNKS - 1:
+                add_on_gpsimd(c)
             prepare(n)
             prepare_gates(n)
-            if c >= LAG and j < LEFT:
-                add_quarter(c - LAG, j)
-            if c >= LAG and j == 0:
-                add_share_blocks(c - LAG)
-            if c >= LAG and j == 2:
-                share_back(c - LAG)
-            if c >= LAG and j == GROUPS - 1:
-                finish(c - LAG)
+            if LAG <= c < CHUNKS - 2:
+                if j < 2:
+                    turn_tasks(c - LAG, j)
+                if j == 0:
+                    add_share_blocks(c - LAG)
+                if j == 2:
+                    tasks_back(c - LAG)
+                    share_back(c - LAG)
+                if j == GROUPS - 1:
+                    finish(c - LAG)
+            elif c == CHUNKS - 2:
+                if j == 0:
+                    turn_tasks(c - 2, 0)
+                    turn_tasks(c - 2, 1)
+                    add_share_blocks(c - 2)
+                elif j == 1:
+                    tasks_back(c - 2)
+                    share_back(c - 2)
+                elif j == 2:
+                    finish(c - 2)
+                    add_share_blocks(c - 1)
+                elif j == 3:
+                    share_back(c - 1)
+                else:
+                    turn_tasks(c - 1, 0)
+                    turn_tasks(c - 1, 1)
+                    tasks_back(c - 1)
+                    finish(c - 1)
+            elif c == CHUNKS - 1:
+                if j == 0:
+                    add_share_blocks(c - 1)
+                elif j == 1:
+                    share_back(c - 1)
+                elif j == 2:
+                    add_last_task(0)
+                    add_last_share(0)
+                    add_last_share(1)
+                elif j == 3:
+                    add_last_task(1)
+                    add_last_share(2)
+                else:
+                    add_last_task(2)
+                    add_last_share(3)
+                    last_back(0)
+                    last_back(1)
+                    turn_tasks(c - 1, 0)
+                    turn_tasks(c - 1, 1)
+                    tasks_back(c - 1)
+                    add_last_task(3)
+                    add_last_share(4)
+                    last_back(2)
+                    last_back(3)
+                    last_back(SHARED)
+                    finish(c - 1)
+                    finish_last()

@@ -41,7 +41,7 @@ LEFT = 4
 HEAD_BANKS = (("flipped", 1), ("z", 2), ("z", 2), ("by_row", 3))
 HEAD_ROWS = 2 * TILES
 LAG = 2
-PE_SLOTS = 3
+PE_SLOTS = 4
 SUM_COLS = TASKS * OUT_COLS
 
 FLOPS = 2 * ROWS * D * GROUPS * N
@@ -70,11 +70,11 @@ def tile_plelayer_pa_t_e_kernel(
                 nc.sync.dma_start(out=rows[:, i : i + step, :], in_=x_by_partition[:, TILES * c + i : TILES * c + i + step, :])
             x_rows[c] = rows
 
+        bias_once = const.tile([1, TASKS * TASK_GATE + SHARE_GATE], BF16)
+        nc.sync.dma_start(out=bias_once[:, 0 : TASKS * TASK_GATE], in_=gb0.rearrange("t s -> (t s)").unsqueeze(0))
+        nc.sync.dma_start(out=bias_once[:, TASKS * TASK_GATE :], in_=gbs.unsqueeze(0))
         load_x(0, pieces=TILES)
 
-        bias_once = const.tile([1, TASKS * TASK_GATE + SHARE_GATE], BF16)
-        nc.scalar.dma_start(out=bias_once[:, 0 : TASKS * TASK_GATE], in_=gb0.rearrange("t s -> (t s)").unsqueeze(0))
-        nc.scalar.dma_start(out=bias_once[:, TASKS * TASK_GATE :], in_=gbs.unsqueeze(0))
         task_gate_pre = const.tile([P, TASKS, ROWS_PER_PARTITION * TASK_GATE], BF16)
         share_gate_pre = const.tile([P, ROWS_PER_PARTITION * SHARE_GATE], BF16)
 
@@ -111,10 +111,6 @@ def tile_plelayer_pa_t_e_kernel(
 
         w_codes = const.tile([P, GROUPS, PASSES, N], U32, align_bytes=64)
         nc.sync.dma_start(
-            out=w_codes[:, 0:TASKS, :, :].rearrange("p t g n -> p (t g) n").bitcast(I32),
-            in_=ew0_words.rearrange("a p n b -> p a (n b)").bitcast(I32),
-        )
-        nc.sync.dma_start(
             out=w_codes[:, SHARED, :, :].bitcast(I32), in_=ews0_words.rearrange("g p n b -> p g (n b)").bitcast(I32)
         )
         w_scales = const.tile([P, GROUPS, PASSES, N], U8, align_bytes=64)
@@ -122,18 +118,22 @@ def tile_plelayer_pa_t_e_kernel(
         nc.vector.memset(w_scales_i32, 0)
         task_scales = ew0_scales.rearrange("a q n -> q a n").bitcast(I32)
         shared_scales = ews0_scales.rearrange("g q n -> q g n").bitcast(I32)
-        for quadrant in range(4):
-            live = slice(32 * quadrant, 32 * quadrant + 4)
-            rows = slice(4 * quadrant, 4 * quadrant + 4)
-            nc.sync.dma_start(
-                out=w_scales_i32[live, 0:TASKS, :, :].rearrange("p t g n -> p (t g) n"), in_=task_scales[rows]
-            )
+        quadrants = [(slice(32 * q, 32 * q + 4), slice(4 * q, 4 * q + 4)) for q in range(4)]
+        for live, rows in quadrants:
             nc.sync.dma_start(out=w_scales_i32[live, SHARED, :, :], in_=shared_scales[rows])
 
         bias_rows = const.tile([P, P], BF16)
         nc.vector.memset(bias_rows[:], 0.0)
         nc.sync.dma_start(out=bias_rows[0:TASKS, :], in_=eb0.rearrange("t u e -> t (u e)"))
         nc.sync.dma_start(out=bias_rows[SHARED : SHARED + 1, :], in_=ebs0.rearrange("u e -> (u e)").unsqueeze(0))
+        nc.sync.dma_start(
+            out=w_codes[:, 0:TASKS, :, :].rearrange("p t g n -> p (t g) n").bitcast(I32),
+            in_=ew0_words.rearrange("a p n b -> p a (n b)").bitcast(I32),
+        )
+        for live, rows in quadrants:
+            nc.sync.dma_start(
+                out=w_scales_i32[live, 0:TASKS, :, :].rearrange("p t g n -> p (t g) n"), in_=task_scales[rows]
+            )
         expert_bias = const.tile([P, GROUPS], F32)
 
         def turn_expert_bias():

from contextlib import ExitStack

import concourse.mybir as mybir
from concourse.masks import make_identity

F32 = mybir.dt.float32
BF16 = mybir.dt.bfloat16
I32 = mybir.dt.int32
U32 = mybir.dt.uint32
U8 = mybir.dt.uint8
FP8X4 = mybir.dt.float8_e4m3fn_x4
ADD = mybir.AluOpType.add
MULT = mybir.AluOpType.mult
MAX = mybir.AluOpType.max
LAST_AXIS = mybir.AxisListType.X
LAST_TWO_AXES = mybir.AxisListType.XY
EXP = mybir.ActivationFunctionType.Exp
RELU = mybir.ActivationFunctionType.Relu
COPY = mybir.ActivationFunctionType.Copy

P = 128
TASKS, ROWS, D, UNITS, EXPERTS = 4, 8192, 1024, 16, 8
GROUPS = TASKS + 1
SHARED = TASKS
N = UNITS * EXPERTS
K_PASS = 4 * P
PASSES = D // K_PASS
WORD_PLANES = 2
TILES = 4
CHUNK = TILES * P
CHUNKS = ROWS // CHUNK
ROWS_PER_PARTITION = ROWS // P
TASK_GATE = 2 * EXPERTS
SHARE_GATE = GROUPS * EXPERTS
TASK_COLS = TASKS * TILES * TASK_GATE
GATE_COLS = TASK_COLS + TILES * SHARE_GATE
SOFTMAXES = TASKS * TILES + TILES
OUT_COLS = TILES * UNITS
ORDER = (SHARED,) + tuple(range(TASKS))
LEFT = 4
HEAD_BANKS = (("flipped", 1), ("z", 2), ("z", 2), ("by_row", 3))
HEAD_ROWS = 2 * TILES
LAG = 2
PE_SLOTS = 4
SUM_COLS = TASKS * OUT_COLS

FLOPS = 2 * ROWS * D * GROUPS * N


def tile_plelayer_pa_t_e_kernel(
    tc, x, ews0_words, ews0_scales, ebs0, ew0_words, ew0_scales, eb0, gate_pre0, gb0, sgate_pre, gbs, out_0, out_1
):
    nc = tc.nc
    with ExitStack() as ctx:
        const = ctx.enter_context(tc.tile_pool(name="const", bufs=1))
        x_pool = ctx.enter_context(tc.tile_pool(name="x_pool", bufs=4))
        mx_pool = ctx.enter_context(tc.tile_pool(name="mx_pool", bufs=3))
        hidden_pool = ctx.enter_context(tc.tile_pool(name="hidden_pool", bufs=4))
        gate_pool = ctx.enter_context(tc.tile_pool(name="gate_pool", bufs=6))
        sum_pool = ctx.enter_context(tc.tile_pool(name="sum_pool", bufs=2))
        psum = ctx.enter_context(tc.psum_pool(name="psum", bufs=1))

        x_by_partition = x.rearrange("(p a) k -> p a k", a=ROWS_PER_PARTITION)
        x_rows = {}

        def load_x(c, pieces=1):
            rows = x_pool.tile([P, TILES, D], BF16)
            step = TILES // pieces
            for i in range(0, TILES, step):
                nc.sync.dma_start(out=rows[:, i : i + step, :], in_=x_by_partition[:, TILES * c + i : TILES * c + i + step, :])
            x_rows[c] = rows

        bias_once = const.tile([1, TASKS * TASK_GATE + SHARE_GATE], BF16)
        nc.sync.dma_start(out=bias_once[:, 0 : TASKS * TASK_GATE], in_=gb0.rearrange("t s -> (t s)").unsqueeze(0))
        nc.sync.dma_start(out=bias_once[:, TASKS * TASK_GATE :], in_=gbs.unsqueeze(0))
        load_x(0, pieces=TILES)

        task_gate_pre = const.tile([P, TASKS, ROWS_PER_PARTITION * TASK_GATE], BF16)
        share_gate_pre = const.tile([P, ROWS_PER_PARTITION * SHARE_GATE], BF16)

        def load_gates(first_row, last_row):
            nc.sync.dma_start(
                out=task_gate_pre[:, :, TASK_GATE * first_row : TASK_GATE * last_row],
                in_=gate_pre0.rearrange("t (p a) s -> p t (a s)", a=ROWS_PER_PARTITION)[
                    :, :, TASK_GATE * first_row : TASK_GATE * last_row
                ],
            )
            nc.sync.dma_start(
                out=share_gate_pre[:, SHARE_GATE * first_row : SHARE_GATE * last_row],
                in_=sgate_pre.rearrange("(p a) s -> p (a s)", a=ROWS_PER_PARTITION)[
                    :, SHARE_GATE * first_row : SHARE_GATE * last_row
                ],
            )

        load_gates(0, HEAD_ROWS)

        ident_f32 = const.tile([P, P], F32)
        make_identity(nc, ident_f32[:])
        ident_bf16 = const.tile([P, P], BF16)
        make_identity(nc, ident_bf16[:])
        ones_bf16 = const.tile([P, P], BF16)
        nc.vector.memset(ones_bf16[:], 1.0)
        expert_major = const.tile([P, P], F32)
        nc.vector.tensor_copy(
            out=expert_major[:].rearrange("p (e u) -> p e u", e=EXPERTS),
            in_=ident_f32[:].rearrange("p (u e) -> p e u", e=EXPERTS),
        )

        fold = const.tile([P, OUT_COLS], F32)
        nc.vector.tensor_tensor(out=fold[:], in0=ident_f32[:, 0:OUT_COLS], in1=ident_f32[:, OUT_COLS:P], op=ADD)

        w_codes = const.tile([P, GROUPS, PASSES, N], U32, align_bytes=64)
        nc.sync.dma_start(
            out=w_codes[:, SHARED, :, :].bitcast(I32), in_=ews0_words.rearrange("g p n b -> p g (n b)").bitcast(I32)
        )
        w_scales = const.tile([P, GROUPS, PASSES, N], U8, align_bytes=64)
        w_scales_i32 = w_scales[:].bitcast(I32)
        nc.vector.memset(w_scales_i32, 0)
        task_scales = ew0_scales.rearrange("a q n -> q a n").bitcast(I32)
        shared_scales = ews0_scales.rearrange("g q n -> q g n").bitcast(I32)
        quadrants = [(slice(32 * q, 32 * q + 4), slice(4 * q, 4 * q + 4)) for q in range(4)]
        for live, rows in quadrants:
            nc.sync.dma_start(out=w_scales_i32[live, SHARED, :, :], in_=shared_scales[rows])

        bias_rows = const.tile([P, P], BF16)
        nc.vector.memset(bias_rows[:], 0.0)
        nc.sync.dma_start(out=bias_rows[0:TASKS, :], in_=eb0.rearrange("t u e -> t (u e)"))
        nc.sync.dma_start(out=bias_rows[SHARED : SHARED + 1, :], in_=ebs0.rearrange("u e -> (u e)").unsqueeze(0))
        nc.sync.dma_start(
            out=w_codes[:, 0:TASKS, :, :].rearrange("p t g n -> p (t g) n").bitcast(I32),
            in_=ew0_words.rearrange("a p n b -> p a (n b)").bitcast(I32),
        )
        for live, rows in quadrants:
            nc.sync.dma_start(
                out=w_scales_i32[live, 0:TASKS, :, :].rearrange("p t g n -> p (t g) n"), in_=task_scales[rows]
            )
        expert_bias = const.tile([P, GROUPS], F32)

        def turn_expert_bias():
            bias_columns = psum.tile([P, P], BF16, tag="by_row", bufs=3)
            nc.tensor.transpose(out=bias_columns[:], in_=bias_rows[:], identity=ident_bf16[:])
            nc.vector.tensor_copy(out=expert_bias[:], in_=bias_columns[:, 0:GROUPS])

        gate_bias = const.tile([P, GATE_COLS], BF16)
        nc.vector.memset(gate_bias[:], 0.0)
        nc.vector.tensor_copy(
            out=gate_bias[0:1, 0:TASK_COLS].rearrange("o (t i s) -> o t i s", t=TASKS, i=TILES),
            in_=bias_once[:, 0 : TASKS * TASK_GATE]
            .rearrange("o (t s) -> o t s", t=TASKS)
            .unsqueeze(2)
            .to_broadcast([1, TASKS, TILES, TASK_GATE]),
        )
        nc.vector.tensor_copy(
            out=gate_bias[0:1, TASK_COLS:GATE_COLS].rearrange("o (i s) -> o i s", i=TILES),
            in_=bias_once[:, TASKS * TASK_GATE :].unsqueeze(1).to_broadcast([1, TILES, SHARE_GATE]),
        )

        bias_everywhere = const.tile([P, GATE_COLS], F32)

        def spread_gate_bias():
            bias_in_psum = psum.tile([P, GATE_COLS], F32, tag="task_sums")
            nc.tensor.matmul(out=bias_in_psum[:], lhsT=ones_bf16[:], rhs=gate_bias[:], start=True, stop=True)
            nc.vector.tensor_copy(out=bias_everywhere[:], in_=bias_in_psum[:])

        logits = const.tile([P, CHUNKS, GATE_COLS], F32)

        def add_gate_bias(first, last):
            count = last - first
            nc.gpsimd.tensor_tensor(
                out=logits[:, first:last, 0:TASK_COLS].rearrange("p c (t n) -> p t c n", t=TASKS),
                in0=task_gate_pre[:, :, TILES * TASK_GATE * first : TILES * TASK_GATE * last].rearrange(
                    "p t (c n) -> p t c n", c=count
                ),
                in1=bias_everywhere[:, 0:TASK_COLS]
                .rearrange("p (t n) -> p t n", t=TASKS)
                .unsqueeze(2)
                .to_broadcast([P, TASKS, count, TILES * TASK_GATE]),
                op=ADD,
            )
            nc.gpsimd.tensor_tensor(
                out=logits[:, first:last, TASK_COLS:GATE_COLS],
                in0=share_gate_pre[:, TILES * SHARE_GATE * first : TILES * SHARE_GATE * last].rearrange(
                    "p (c n) -> p c n", c=count
                ),
                in1=bias_everywhere[:, TASK_COLS:GATE_COLS].unsqueeze(1).to_broadcast([P, count, TILES * SHARE_GATE]),
                op=ADD,
            )

        task_out_by_partition = out_0.rearrange("t (p a) u -> p t a u", a=ROWS_PER_PARTITION)
        share_out_by_partition = out_1.rearrange("(p a) u -> p a u", a=ROWS_PER_PARTITION)

        grouped, x_codes, x_scales, hidden, experts_by_row = {}, {}, {}, {}, {}
        minus_max, gates, gate_sums = {}, {}, {}
        task_products, share_products, task_quarters, task_sums, share_sums = {}, {}, {}, {}, {}

        def transpose_x(c, i):
            if i == 0:
                side_by_side = mx_pool.tile([P, PASSES * CHUNK * 4], BF16, align_bytes=64)
                grouped[c] = side_by_side
            words = x_rows[c][:, i, :].bitcast(F32)
            tag, bufs = HEAD_BANKS[i] if c == 0 else HEAD_BANKS[0]
            flipped = psum.tile([P, PASSES * WORD_PLANES, P], F32, tag=tag, bufs=bufs)
            for g in range(PASSES):
                for h in range(WORD_PLANES):
                    first = (K_PASS // 2) * g + h
                    nc.tensor.transpose(
                        out=flipped[:, WORD_PLANES * g + h, :],
                        in_=words[:, first : (K_PASS // 2) * (g + 1) : WORD_PLANES],
                        identity=ident_f32[:],
                    )
            nc.scalar.copy(
                out=grouped[c][:]
                .bitcast(F32)
                .rearrange("p (g n h) -> p g n h", g=PASSES, h=WORD_PLANES)[:, :, P * i : P * (i + 1), :],
                in_=flipped[:].rearrange("p (g h) n -> p g n h", h=WORD_PLANES),
            )

        def quantise_x(c, pieces=1):
            codes = mx_pool.tile([P, PASSES * CHUNK], U32, align_bytes=64)
            scales = mx_pool.tile([P, PASSES * CHUNK], U8, align_bytes=64)
            width = PASSES * CHUNK if pieces == 1 else P
            for first in range(0, CHUNK, CHUNK // pieces):
                for g in range(1 if pieces == 1 else PASSES):
                    columns = slice(CHUNK * g + first, CHUNK * g + first + width)
                    nc.vector.quantize_mx(
                        out=codes[:, columns].bitcast(FP8X4),
                        scales=scales[:, columns],
                        in_=grouped[c][:, 4 * columns.start : 4 * columns.stop],
                    )
            x_codes[c] = codes
            x_scales[c] = scales

        def run_experts(c, w):
            z = psum.tile([P, CHUNK], F32, tag="z", bufs=2)
            for g in range(PASSES):
                columns = slice(CHUNK * g, CHUNK * (g + 1))
                nc.tensor.matmul_mx(
                    out=z[:],
                    lhsT=w_codes[:, w, g, :].bitcast(FP8X4),
                    lhsT_scale=w_scales[:, w, g, :],
                    rhs=x_codes[c][:, columns].bitcast(FP8X4),
                    rhs_scale=x_scales[c][:, columns],
                    start=(g == 0),
                    stop=(g == PASSES - 1),
                )
            active = hidden_pool.tile([P, CHUNK], F32)
            nc.scalar.activation(out=active[:], in_=z[:], func=RELU, bias=expert_bias[:, w : w + 1], scale=1.0)
            hidden[c, w] = active

        def gate_maxima(c):
            negated = gate_pool.tile([P, SOFTMAXES], F32)
            nc.vector.tensor_reduce(
                out=negated[:, 0 : TASKS * TILES],
                in_=logits[:, c, 0:TASK_COLS].rearrange("p (a s) -> p a s", s=TASK_GATE),
                axis=LAST_AXIS,
                op=MAX,
                negate=True,
            )
            nc.vector.tensor_reduce(
                out=negated[:, TASKS * TILES : SOFTMAXES],
                in_=logits[:, c, TASK_COLS:GATE_COLS].rearrange("p (a s) -> p a s", s=SHARE_GATE),
                axis=LAST_AXIS,
                op=MAX,
                negate=True,
            )
            weights = gate_pool.tile([P, GATE_COLS], F32)
            sums = gate_pool.tile([P, SOFTMAXES], F32)
            minus_max[c], gates[c], gate_sums[c] = negated, weights, sums

        def exponentiate(c, w):
            width = SHARE_GATE if w == SHARED else TASK_GATE
            for i in range(TILES):
                a = TILES * w + i
                first = TILES * TASK_GATE * w + width * i
                nc.scalar.activation(
                    out=gates[c][:, first : first + width],
                    in_=logits[:, c, first : first + width],
                    func=EXP,
                    bias=minus_max[c][:, a : a + 1],
                    scale=1.0,
                    accum_out=gate_sums[c][:, a : a + 1],
                )

        def gate_entries(c, first_col, width, first_entry):
            by_tile = gates[c][:, first_col : first_col + TILES * width].rearrange("p (i s) -> p i s", s=width)
            return by_tile[:, :, first_entry : first_entry + EXPERTS]

        def rows_back(c, j):
            by_row = psum.tile([P, TILES, N], F32, tag="by_row", bufs=3)
            for i in range(TILES):
                nc.tensor.transpose(
                    out=by_row[:, i, :], in_=hidden[c, ORDER[j]][:, P * i : P * (i + 1)], identity=expert_major[:]
                )
            experts_by_row[c, j] = by_row

        def last_task_slots(c):
            return task_products[c][:].rearrange("p e k t n -> p (e k t n)").rearrange(
                "p (k t e n) -> p k t e n", k=2, t=TASKS, e=EXPERTS
            )

        def weigh_experts(c, j):
            w = ORDER[j]
            if j == 0:
                for_tasks = sum_pool.tile([P, EXPERTS, 2, TASKS, OUT_COLS], F32)
                for_share = sum_pool.tile([P, GROUPS, TILES * N], F32, bufs=LAG + 1)
                task_products[c], share_products[c] = for_tasks, for_share
            last = c == CHUNKS - 1
            experts_first = experts_by_row[c, j][:].rearrange("p i (e u) -> p e i u", e=EXPERTS)

            def multiply(out, entries):
                nc.vector.tensor_tensor(
                    out=out.rearrange("p e (i u) -> p e i u", u=UNITS),
                    in0=experts_first,
                    in1=entries.rearrange("p i e -> p e i").unsqueeze(3).to_broadcast([P, EXPERTS, TILES, UNITS]),
                    op=MULT,
                )

            def for_task(t, own_or_shared):
                by_slot = last_task_slots(c)[:, own_or_shared, t, :, :] if last else task_products[c][:, :, own_or_shared, t, :]
                multiply(
                    by_slot,
                    gate_entries(c, TILES * TASK_GATE * t, TASK_GATE, EXPERTS * own_or_shared),
                )

            if w == SHARED:
                for t in range(TASKS):
                    for_task(t, 1)
            else:
                for_task(w, 0)
            if j < PE_SLOTS or last:
                multiply(
                    share_products[c][:, j, :].rearrange("p (e n) -> p e n", e=EXPERTS),
                    gate_entries(c, TASK_COLS, SHARE_GATE, EXPERTS * w),
                )
            else:
                nc.vector.tensor_tensor(
                    out=share_products[c][:, j, :].rearrange("p (i u e) -> p i u e", i=TILES, e=EXPERTS),
                    in0=experts_by_row[c, j][:].rearrange("p i (e u) -> p i u e", e=EXPERTS),
                    in1=gate_entries(c, TASK_COLS, SHARE_GATE, EXPERTS * w)
                    .unsqueeze(2)
                    .to_broadcast([P, TILES, UNITS, EXPERTS]),
                    op=MULT,
                )

        def add_on_gpsimd(c):
            products = task_products[c][:].rearrange("p e k t n -> p e (k t n)")
            half = sum_pool.tile([P, EXPERTS // 2, 2 * TASKS * OUT_COLS], F32)
            nc.gpsimd.tensor_tensor(
                out=half[:], in0=products[:, 0 : EXPERTS // 2, :], in1=products[:, EXPERTS // 2 :, :], op=ADD
            )
            quarter = sum_pool.tile([P, EXPERTS // 4, 2 * TASKS * OUT_COLS], F32)
            nc.gpsimd.tensor_tensor(
                out=quarter[:], in0=half[:, 0 : EXPERTS // 4, :], in1=half[:, EXPERTS // 4 :, :], op=ADD
            )
            task_quarters[c] = quarter

        def turn_tasks(c, half):
            if half == 0:
                totals = psum.tile([P, 2 * SUM_COLS], F32, tag="task_sums")
                task_sums[c] = totals
            blocks = task_quarters[c][:].rearrange("p e (k h m) -> p (e k) h m", k=2, m=P)
            for r in range(LEFT):
                nc.tensor.matmul(
                    out=task_sums[c][:, P * half : P * (half + 1)], lhsT=blocks[:, r, half, :], rhs=ident_f32[:],
                    is_transpose=True, start=(r == 0), stop=(r == LEFT - 1),
                )

        def tasks_back(c):
            turned = sum_pool.tile([P, SUM_COLS], F32)
            nc.scalar.copy(out=turned[:], in_=task_sums[c][:, 0:SUM_COLS])
            for first in range(0, SUM_COLS, P):
                nc.tensor.transpose(
                    out=task_sums[c][:, SUM_COLS + first : SUM_COLS + first + P],
                    in_=turned[:, first : first + P],
                    identity=ident_f32[:],
                )

        def add_share_blocks(c):
            sums = psum.tile([P, P + OUT_COLS], F32, tag="flipped" if c == CHUNKS - 3 else "share_sums")
            share_sums[c] = sums
            blocks = share_products[c][:].rearrange("p s (b m) -> p (s b) m", m=P)
            count = PE_SLOTS * TILES * N // P
            for b in range(count):
                nc.tensor.matmul(
                    out=sums[:, 0:P], lhsT=blocks[:, b, :], rhs=ident_f32[:], is_transpose=True,
                    start=(b == 0), stop=(b == count - 1),
                )

        def share_back(c):
            in_sbuf = sum_pool.tile([P, P], F32)
            nc.scalar.copy(out=in_sbuf[:], in_=share_sums[c][:, 0:P])
            nc.tensor.matmul(out=share_sums[c][:, P:], lhsT=in_sbuf[:], rhs=fold[:], start=True, stop=True)

        def finish(c):
            one_over = gate_pool.tile([P, SOFTMAXES], F32)
            nc.vector.reciprocal(out=one_over[:], in_=gate_sums[c][:])
            outputs = sum_pool.tile([P, SUM_COLS + OUT_COLS], F32)
            nc.vector.tensor_tensor(
                out=outputs[:, 0:SUM_COLS].rearrange("p (a u) -> p a u", u=UNITS),
                in0=task_sums[c][:, SUM_COLS:].rearrange("p (a u) -> p a u", u=UNITS),
                in1=one_over[:, 0 : TASKS * TILES].unsqueeze(2).to_broadcast([P, TASKS * TILES, UNITS]),
                op=MULT,
            )
            reduced = sum_pool.tile([P, OUT_COLS], F32)
            nc.vector.tensor_reduce(
                out=reduced[:],
                in_=share_products[c][:, PE_SLOTS:GROUPS, :].rearrange("p s (n e) -> p n s e", e=EXPERTS),
                axis=LAST_TWO_AXES,
                op=ADD,
            )
            both = sum_pool.tile([P, OUT_COLS], F32)
            nc.vector.tensor_tensor(out=both[:], in0=share_sums[c][:, P:], in1=reduced[:], op=ADD)
            for i in range(TILES):
                units = slice(UNITS * i, UNITS * (i + 1))
                nc.scalar.activation(
                    out=outputs[:, SUM_COLS + UNITS * i : SUM_COLS + UNITS * (i + 1)],
                    in_=both[:, units],
                    func=COPY,
                    scale=one_over[:, TASKS * TILES + i : TASKS * TILES + i + 1],
                )
            store(c, outputs)

        def store(c, outputs):
            own_rows = slice(TILES * c, TILES * (c + 1))
            nc.sync.dma_start(
                out=task_out_by_partition[:, :, own_rows, :],
                in_=outputs[:, 0:SUM_COLS].rearrange("p (t i u) -> p t i u", t=TASKS, i=TILES),
            )
            nc.sync.dma_start(
                out=share_out_by_partition[:, own_rows, :],
                in_=outputs[:, SUM_COLS:].rearrange("p (i u) -> p i u", u=UNITS),
            )

        last_sums_in_psum = {}

        def add_blocks(out, products, first, last):
            blocks = products.rearrange("p (b m) -> p b m", m=P)
            for b in range(EXPERTS // 2):
                nc.tensor.matmul(
                    out=out, lhsT=blocks[:, b, :], rhs=ident_f32[:], is_transpose=True,
                    start=(first and b == 0), stop=(last and b == EXPERTS // 2 - 1),
                )

        def add_last_task(t):
            c = CHUNKS - 1
            if t == 0:
                by_task = psum.tile([P, TASKS, P], F32, tag="flipped")
                last_sums_in_psum["tasks"] = by_task
            for k in (1, 0):
                add_blocks(
                    last_sums_in_psum["tasks"][:, t, :],
                    last_task_slots(c)[:, k, t, :, :].rearrange("p e n -> p (e n)"),
                    first=(k == 1),
                    last=(k == 0),
                )

        def add_last_share(j):
            if j == 0:
                by_share = psum.tile([P, P], F32, tag="z", bufs=2)
                last_sums_in_psum["share"] = by_share
            add_blocks(
                last_sums_in_psum["share"][:], share_products[CHUNKS - 1][:, j, :], first=(j == 0), last=(j == GROUPS - 1)
            )

        def last_back(a):
            if a == 0:
                totals = psum.tile([P, GROUPS, OUT_COLS], F32, tag="z", bufs=2)
                last_sums_in_psum["all"] = totals
            in_sbuf = sum_pool.tile([P, P], F32)
            source = last_sums_in_psum["share"][:] if a == SHARED else last_sums_in_psum["tasks"][:, a, :]
            nc.scalar.copy(out=in_sbuf[:], in_=source)
            nc.tensor.matmul(out=last_sums_in_psum["all"][:, a, :], lhsT=in_sbuf[:], rhs=fold[:], start=True, stop=True)

        def finish_last():
            c = CHUNKS - 1
            one_over = gate_pool.tile([P, SOFTMAXES], F32)
            nc.vector.reciprocal(out=one_over[:], in_=gate_sums[c][:])
            outputs = sum_pool.tile([P, SUM_COLS + OUT_COLS], F32)
            nc.vector.tensor_tensor(
                out=outputs[:].rearrange("p (a u) -> p a u", u=UNITS),
                in0=last_sums_in_psum["all"][:].rearrange("p a (i u) -> p (a i) u", u=UNITS),
                in1=one_over[:].unsqueeze(2).to_broadcast([P, SOFTMAXES, UNITS]),
                op=MULT,
            )
            store(c, outputs)

        STEPS = CHUNKS * GROUPS

        def feed(n):
            if n < STEPS:
                run_experts(n // GROUPS, ORDER[n % GROUPS])

        def prepare(n):
            c, phase = (n + 11) // GROUPS, (n + 11) % GROUPS
            if c >= CHUNKS:
                return
            if phase < TILES:
                transpose_x(c, phase)
            else:
                quantise_x(c)

        def prepare_gates(n):
            c, w = (n + 6) // GROUPS, (n + 6) % GROUPS
            if c >= CHUNKS:
                return
            if w == 0:
                gate_maxima(c)
            exponentiate(c, w)

        load_x(1)
        load_gates(HEAD_ROWS, ROWS_PER_PARTITION)
        load_x(2)
        transpose_x(0, 0)
        transpose_x(0, 1)
        spread_gate_bias()
        transpose_x(0, 2)
        transpose_x(0, 3)
        add_gate_bias(0, 1)
        quantise_x(0, pieces=TILES)
        gate_maxima(0)
        turn_expert_bias()
        feed(0)
        for w in range(GROUPS):
            exponentiate(0, w)
        rows_back(0, 0)
        feed(1)
        for first, last in ((1, 4), (4, 9), (9, CHUNKS)):
            add_gate_bias(first, last)
        prepare_gates(-1)
        for n in range(-6, 0):
            prepare(n)
        for n in range(STEPS):
            c, j = n // GROUPS, n % GROUPS
            if j == 0 and c + 3 < CHUNKS:
                load_x(c + 3)
            if c < CHUNKS - 2:
                feed(n + 2)
            else:
                if n == (CHUNKS - 2) * GROUPS:
                    feed(n + 2)
                feed(n + 3)
            if n + 1 < STEPS:
                rows_back((n + 1) // GROUPS, (n + 1) % GROUPS)
            weigh_experts(c, j)
            if j == GROUPS - 1 and c < CHUNKS - 1:
                add_on_gpsimd(c)
            prepare(n)
            prepare_gates(n)
            if LAG <= c < CHUNKS - 2:
                if j < 2:
                    turn_tasks(c - LAG, j)
                if j == 0:
                    add_share_blocks(c - LAG)
                if j == 2:
                    tasks_back(c - LAG)
                    share_back(c - LAG)
                if j == GROUPS - 1:
                    finish(c - LAG)
            elif c == CHUNKS - 2:
                if j == 0:
                    turn_tasks(c - 2, 0)
                    turn_tasks(c - 2, 1)
                    add_share_blocks(c - 2)
                elif j == 1:
                    tasks_back(c - 2)
                    share_back(c - 2)
                elif j == 2:
                    finish(c - 2)
                    add_share_blocks(c - 1)
                elif j == 3:
                    share_back(c - 1)
                else:
                    turn_tasks(c - 1, 0)
                    turn_tasks(c - 1, 1)
                    tasks_back(c - 1)
                    finish(c - 1)
            elif c == CHUNKS - 1:
                if j == 0:
                    add_share_blocks(c - 1)
                elif j == 1:
                    share_back(c - 1)
                elif j == 2:
                    add_last_task(0)
                    add_last_share(0)
                    add_last_share(1)
                elif j == 3:
                    add_last_task(1)
                    add_last_share(2)
                else:
                    add_last_task(2)
                    add_last_share(3)
                    last_back(0)
                    last_back(1)
                    turn_tasks(c - 1, 0)
                    turn_tasks(c - 1, 1)
                    tasks_back(c - 1)
                    add_last_task(3)
                    add_last_share(4)
                    last_back(2)
                    last_back(3)
                    last_back(SHARED)
                    finish(c - 1)
                    finish_last()
